import numpy as np
import ml_dtypes


def mxq(x, axis, fmt="e4m3"):
    dtype, down = {"e4m3": (ml_dtypes.float8_e4m3fn, 7), "e5m2": (ml_dtypes.float8_e5m2, 14)}[fmt]
    v = np.moveaxis(np.asarray(x, np.float32).astype(ml_dtypes.bfloat16).astype(np.float64), axis, -1)
    blocks = v.reshape(v.shape[:-1] + (-1, 32))
    amax = np.abs(blocks).max(-1, keepdims=True)
    byte = np.maximum(np.where(amax > 0, np.frexp(amax)[1] - 1 + 127, 0) - down, 1)
    scale = np.exp2(byte - 127.0)
    codes = (blocks / scale).astype(np.float32).astype(dtype).astype(np.float64)
    return np.moveaxis((codes * scale).reshape(v.shape), -1, axis)


WIDE = False


def mx_kscale(k):
    if not WIDE:
        return np.ones(k)
    levels = np.array([20, -20, 10, -10, 0])
    a = np.random.permutation(np.resize(levels, k // 512 * 4)).reshape(k // 512, 4)
    idx = np.arange(k)
    return np.exp2(a[idx // 512, idx % 128 // 32])


BF16 = ml_dtypes.bfloat16


def bf(x):
    return np.asarray(x, np.float32).astype(BF16)


def f64(x):
    return np.asarray(x).astype(np.float64)


B, IN_C, OUT_C, HM, HN, NL = 512, 512, 512, 512, 8, 3
K = HN * HM


def leaky(v, leak):
    return np.where(v < 0, v * leak, v)


def setup_inputs():
    u = mx_kscale(K).reshape(HN, HM)
    x = bf(np.random.standard_normal((B, IN_C)))
    wim0 = bf(np.random.standard_normal((HN, IN_C, HM)) * 0.7 / np.sqrt(IN_C))
    win0 = bf(np.random.standard_normal((HM, IN_C, HN)) * 0.7 / np.sqrt(IN_C))
    leak_m = bf(np.random.uniform(-2.0, 2.0, HM))
    leak_n = bf(np.random.uniform(-2.0, 2.0, HN))
    g = bf(np.random.standard_normal((B, HN, HM)) * np.exp2(np.random.randint(-12, 1, (B, 1, 1))) * 16.0 * u[None, :, :])
    z_m = (f64(x) @ f64(wim0).transpose(1, 0, 2).reshape(IN_C, HN * HM)).reshape(B, HN, HM)
    z_n = (f64(x) @ f64(win0).transpose(1, 0, 2).reshape(IN_C, HM * HN)).reshape(B, HM, HN)
    return {"x": x,
            "W_im": bf(f64(wim0) / u[:, None, :]),
            "W_in": bf(f64(win0) / u.T[:, None, :]),
            "leak_m": leak_m,
            "leak_n": leak_n,
            "z_m": np.asarray(z_m, np.float32),
            "z_n": np.asarray(z_n, np.float32),
            "grad_out": g}


def reference(x, W_im, W_in, leak_m, leak_n, z_m, z_n, grad_out):
    g = f64(grad_out)
    dm = g * np.where(f64(z_m) < 0, f64(leak_m), 1.0)
    dn = g * np.where(f64(z_n) < 0, f64(leak_n), 1.0).transpose(0, 2, 1)
    dmq = mxq(dm.reshape(B, K), 1, "e5m2")
    dnq = mxq(dn.reshape(B, K), 1, "e5m2")
    wim = mxq(f64(W_im).transpose(0, 2, 1).reshape(K, IN_C), 0, "e4m3")
    win = mxq(f64(W_in).transpose(2, 0, 1).reshape(K, IN_C), 0, "e4m3")
    return (dmq @ wim) + (dnq @ win)

@@ -1,0 +1,290 @@
+import concourse.mybir as mybir
+from concourse.masks import make_identity
+
+F32 = mybir.dt.float32
+BF16 = mybir.dt.bfloat16
+U32 = mybir.dt.uint32
+U8 = mybir.dt.uint8
+E4M3_X4 = mybir.dt.float8_e4m3fn_x4
+E5M2_X4 = mybir.dt.float8_e5m2_x4
+ALU = mybir.AluOpType
+ACT = mybir.ActivationFunctionType
+
+P = 128
+B, IN_C, HM, HN = 512, 512, 512, 8
+PACK = 4
+B_TILES = B // P
+HALF_N = HN // 2
+STAGES = 2 * B_TILES
+STAGE = HALF_N * P
+I_CHUNKS = 4
+I_CHUNK = IN_C // I_CHUNKS
+N_PAIRS = HN // 2
+
+FLOPS = 2 * 2 * B * IN_C * HN * HM
+BYTES = 2 * (2 * HN * IN_C * HM) + 2 * (4 * B * HN * HM) + 2 * B * HN * HM + 4 * B * IN_C
+
+
+def tile_tensormoe_pa_v_kernel(tc, x, W_im, W_in, leak_m, leak_n, z_m, z_n, grad_out, out):
+    nc = tc.nc
+    with (
+        tc.tile_pool(name="const", bufs=1) as const,
+        tc.tile_pool(name="weights", bufs=1) as weights,
+        tc.tile_pool(name="wstage", bufs=2) as wstage,
+        tc.tile_pool(name="loads", bufs=2) as loads,
+        tc.tile_pool(name="work", bufs=2) as work,
+        tc.psum_pool(name="tpsum", bufs=6) as tpsum,
+        tc.psum_pool(name="accs", bufs=2) as accs,
+        tc.manual_schedule(),
+    ):
+
+        lm_bf = const.tile([P, PACK], BF16)
+        nc.gpsimd.dma_start(
+            out=lm_bf[:].rearrange("q (u e) -> q u e", u=2),
+            in_=leak_m.rearrange("(u q e) -> q u e", u=2, e=2),
+        )
+        ln_bf = const.tile([P, HN], BF16)
+        nc.gpsimd.dma_start(out=ln_bf[:], in_=leak_n.partition_broadcast(P))
+        ident = const.tile([P, P], F32)
+        make_identity(nc, ident[:])
+
+        wim_codes = weights.tile([P, HN, IN_C], U32, align_bytes=64)
+        wim_scales = weights.tile([P, HN, IN_C], U8, align_bytes=64)
+        win_codes = weights.tile([P, HN, IN_C], U32, align_bytes=64)
+        win_scales = weights.tile([P, HN, IN_C], U8, align_bytes=64)
+
+        def load_rows(j):
+            rows = slice(j * P, (j + 1) * P)
+            zn_halves = []
+            for u in range(2):
+                zn = loads.tile([P, HM // 2 * HN], F32, tag="z", bufs=6, name="zn")
+                m_range = slice(u * (HM // 2), (u + 1) * (HM // 2))
+                nc.sync.dma_start(out=zn[:], in_=z_n[rows, m_range, :].rearrange("b m n -> b (m n)"))
+                zn_halves.append(zn)
+            g = loads.tile([P, HN * HM], BF16, name="g")
+            nc.sync.dma_start(out=g[:], in_=grad_out[rows].rearrange("b n m -> b (n m)"))
+            zm_halves = []
+            for h in range(2):
+                zm = loads.tile([P, HALF_N * HM], F32, tag="z", bufs=6, name="zm")
+                n_range = slice(h * HALF_N, (h + 1) * HALF_N)
+                nc.sync.dma_start(out=zm[:], in_=z_m[rows, n_range, :].rearrange("b n m -> b (n m)"))
+                zm_halves.append(zm)
+            return zn_halves, g, zm_halves
+
+        win_rows = W_in.rearrange("(u q e) i n -> u q e (i n)", u=2, e=2)
+        win_raws = []
+        for c in range(I_CHUNKS):
+            win_raw = wstage.tile([P, PACK, I_CHUNK, HN], BF16, tag="raw", bufs=4, name="win_raw")
+            for u in range(2):
+                nc.sync.dma_start(
+                    out=win_raw[:, 2 * u : 2 * u + 2].rearrange("q e i n -> q e (i n)"),
+                    in_=win_rows[u, :, :, c * I_CHUNK * HN : (c + 1) * I_CHUNK * HN],
+                )
+            win_raws.append(win_raw)
+        loaded = {0: load_rows(0)}
+
+        def regroup_win(c):
+            win_grouped = wstage.tile([P, HN, I_CHUNK, PACK], BF16, tag="grouped", bufs=3, name="win_grouped", align_bytes=64)
+            for half in range(2):
+                n_range = slice(half * HALF_N, (half + 1) * HALF_N)
+                dst = win_grouped[:, n_range].rearrange("q n i t -> q i t n")
+                src = win_raws[c][:, :, :, n_range].rearrange("q t i n -> q i t n")
+                if c % 2 == 0:
+                    nc.vector.tensor_copy(out=dst, in_=src)
+                else:
+                    nc.scalar.copy(out=dst, in_=src)
+            return win_grouped
+
+        def quantise_win(c, win_grouped):
+            i_cols = slice(c * I_CHUNK, (c + 1) * I_CHUNK)
+            for n in range(HN):
+                nc.vector.quantize_mx(
+                    out=win_codes[:, n, i_cols].bitcast(E4M3_X4),
+                    scales=win_scales[:, n, i_cols],
+                    in_=win_grouped[:, n].rearrange("q i t -> q (i t)"),
+                )
+
+        from_scalar = {}
+        for c in range(0, I_CHUNKS, 2):
+            from_vector = regroup_win(c)
+            from_scalar[c + 1] = regroup_win(c + 1)
+            quantise_win(c, from_vector)
+        for c in range(1, I_CHUNKS, 2):
+            quantise_win(c, from_scalar[c])
+
+        wim_raws = []
+        for a in range(N_PAIRS):
+            wim_raw = wstage.tile([P, 2 * IN_C // P, HM], BF16, tag="raw", bufs=4, name="wim_raw")
+            nc.sync.dma_start(out=wim_raw[:], in_=W_im[2 * a : 2 * a + 2].rearrange("n (c p) m -> p (n c) m", p=P))
+            wim_raws.append(wim_raw)
+
+        def prepare_wim(a):
+            wim_words = wim_raws[a][:].rearrange("p c m -> p (c m)").bitcast(F32).rearrange("p (c w) -> p c w", w=HM // 2)
+            wim_grouped = wstage.tile([P, 2 * IN_C * PACK], BF16, tag="grouped", bufs=3, name="wim_grouped", align_bytes=64)
+            grouped_words = wim_grouped[:].bitcast(F32).rearrange("q (i u) -> q i u", u=2)
+            for i_half in range(4):
+                bank = tpsum.tile([P, 2, 2 * P], F32, tag="bank", name="wim_bank")
+                for u in range(2):
+                    for cc in range(2):
+                        nc.tensor.transpose(
+                            out=bank[:, u, cc * P : (cc + 1) * P],
+                            in_=wim_words[:, 2 * i_half + cc, u * P : (u + 1) * P],
+                            identity=ident[:],
+                        )
+                dst = grouped_words[:, i_half * 2 * P : (i_half + 1) * 2 * P, :]
+                src = bank[:].rearrange("q u i -> q i u")
+                if i_half % 2 == 0:
+                    nc.scalar.copy(out=dst, in_=src)
+                else:
+                    nc.vector.tensor_copy(out=dst, in_=src)
+            nc.vector.quantize_mx(
+                out=wim_codes[:, 2 * a : 2 * a + 2, :].rearrange("q n i -> q (n i)").bitcast(E4M3_X4),
+                scales=wim_scales[:, 2 * a : 2 * a + 2, :].rearrange("q n i -> q (n i)"),
+                in_=wim_grouped[:],
+            )
+
+        lm = const.tile([P, PACK], F32)
+        one_minus_lm = const.tile([P, PACK], F32)
+        ln = const.tile([P, HN], F32)
+        one_minus_ln = const.tile([P, HN], F32)
+        nc.vector.tensor_copy(out=lm[:], in_=lm_bf[:])
+        nc.vector.tensor_copy(out=ln[:], in_=ln_bf[:])
+        nc.vector.tensor_scalar(out=one_minus_lm[:], in0=lm[:], scalar1=-1.0, scalar2=1.0, op0=ALU.mult, op1=ALU.add)
+        nc.vector.tensor_scalar(out=one_minus_ln[:], in0=ln[:], scalar1=-1.0, scalar2=1.0, op0=ALU.mult, op1=ALU.add)
+
+        pos_ns = {}
+        fronts = {}
+        codes = {}
+        acc_of = {}
+
+        def front(s):
+            j, h = divmod(s, 2)
+            zn_halves, g, zm_halves = loaded[j]
+            if h == 0:
+                pos_n = work.tile([P, HN, HM], BF16, name="pos_n")
+                for u in range(2):
+                    m_range = slice(u * (HM // 2), (u + 1) * (HM // 2))
+                    nc.vector.tensor_single_scalar(
+                        out=pos_n[:, :, m_range].rearrange("b (hh nq) m -> b hh m nq", hh=2),
+                        in_=zn_halves[u][:].rearrange("b (m hh nq) -> b hh m nq", hh=2, nq=HALF_N),
+                        scalar=0.0,
+                        op=ALU.is_ge,
+                    )
+                pos_ns[j] = pos_n
+            pos_m = work.tile([P, HALF_N * HM], BF16, name="pos_m")
+            nc.vector.tensor_single_scalar(out=pos_m[:], in_=zm_halves[h][:], scalar=0.0, op=ALU.is_ge)
+
+            g_words = g[:].bitcast(F32)
+            pos_n_words = pos_ns[j][:].rearrange("b n m -> b (n m)").bitcast(F32)
+            pos_m_words = pos_m[:].bitcast(F32)
+
+            gT = work.tile([P, STAGE * PACK], BF16, name="gT")
+            gT_words = gT[:].bitcast(F32).rearrange("q (nq b u) -> q nq b u", nq=HALF_N, u=2)
+            fnT = work.tile([P, STAGE * PACK], BF16, name="fnT")
+            fnT_view = fnT[:].rearrange("q (nq b u e) -> q nq b u e", nq=HALF_N, u=2, e=2)
+            for pair in range(HALF_N // 2):
+                g_bank = tpsum.tile([P, 2, 2, P], F32, tag="bank", name="g_bank")
+                n_bank = tpsum.tile([P, 2, 2, P], F32, tag="bank", name="n_bank")
+                for bank, words_of in ((g_bank, g_words), (n_bank, pos_n_words)):
+                    for nn in range(2):
+                        n = h * HALF_N + 2 * pair + nn
+                        for u in range(2):
+                            words = slice(n * 2 * P + u * P, n * 2 * P + (u + 1) * P)
+                            nc.tensor.transpose(out=bank[:, nn, u, :], in_=words_of[:, words], identity=ident[:])
+                nc.scalar.copy(
+                    out=gT_words[:, 2 * pair : 2 * pair + 2],
+                    in_=g_bank[:].rearrange("q nn u b -> q nn b u"),
+                )
+                n_bank_bf = n_bank[:].rearrange("q nn u b -> q (nn u b)").bitcast(BF16).rearrange(
+                    "q (nn u b e) -> q nn b u e", nn=2, u=2, e=2
+                )
+                for nn in range(2):
+                    n = h * HALF_N + 2 * pair + nn
+                    nc.scalar.activation(
+                        out=fnT_view[:, 2 * pair + nn],
+                        in_=n_bank_bf[:, nn],
+                        func=ACT.Identity,
+                        scale=one_minus_ln[:, n : n + 1],
+                        bias=ln[:, n : n + 1],
+                    )
+
+            fmT = work.tile([P, PACK, STAGE], BF16, name="fmT")
+            for u in range(2):
+                m_bank = tpsum.tile([P, HALF_N, P], F32, tag="bank", name="m_bank")
+                for nq in range(HALF_N):
+                    words = slice(nq * 2 * P + u * P, nq * 2 * P + (u + 1) * P)
+                    nc.tensor.transpose(out=m_bank[:, nq, :], in_=pos_m_words[:, words], identity=ident[:])
+                m_bank_bf = m_bank[:].rearrange("q nq b -> q (nq b)").bitcast(BF16).rearrange("q (x e) -> q x e", e=2)
+                for e in range(2):
+                    t = 2 * u + e
+                    nc.scalar.activation(
+                        out=fmT[:, t, :],
+                        in_=m_bank_bf[:, :, e],
+                        func=ACT.Identity,
+                        scale=one_minus_lm[:, t : t + 1],
+                        bias=lm[:, t : t + 1],
+                    )
+            fronts[s] = (gT, fnT, fmT)
+            if h == 0 and j + 1 < B_TILES:
+                loaded[j + 1] = load_rows(j + 1)
+
+        def middle(s):
+            gT, fnT, fmT = fronts[s]
+            dnT = work.tile([P, STAGE * PACK], BF16, name="dnT", bufs=1, align_bytes=64)
+            dmT = work.tile([P, STAGE * PACK], BF16, name="dmT", bufs=1, align_bytes=64)
+            nc.vector.tensor_tensor(out=dnT[:], in0=fnT[:], in1=gT[:], op=ALU.mult)
+            nc.vector.tensor_tensor(
+                out=dmT[:].rearrange("q (x t) -> q x t", t=PACK),
+                in0=fmT[:].rearrange("q t x -> q x t"),
+                in1=gT[:].rearrange("q (x t) -> q x t", t=PACK),
+                op=ALU.mult,
+            )
+            dn_codes = work.tile([P, STAGE], U32, name="dn_codes", align_bytes=64)
+            dn_scales = work.tile([P, STAGE], U8, name="dn_scales", align_bytes=64)
+            dm_codes = work.tile([P, STAGE], U32, name="dm_codes", align_bytes=64)
+            dm_scales = work.tile([P, STAGE], U8, name="dm_scales", align_bytes=64)
+            nc.vector.quantize_mx(out=dn_codes[:].bitcast(E5M2_X4), scales=dn_scales[:], in_=dnT[:])
+            nc.vector.quantize_mx(out=dm_codes[:].bitcast(E5M2_X4), scales=dm_scales[:], in_=dmT[:])
+            codes[s] = ((dn_codes, dn_scales, win_codes, win_scales), (dm_codes, dm_scales, wim_codes, wim_scales))
+
+        def back(s):
+            j, h = divmod(s, 2)
+            if h == 0:
+                acc_of[j] = accs.tile([P, IN_C], F32, name="acc")
+            acc = acc_of[j]
+            for product in range(2):
+                d_codes, d_scales, w_codes, w_scales = codes[s][product]
+                for nq in range(HALF_N):
+                    n = h * HALF_N + nq
+                    b_cols = slice(nq * P, (nq + 1) * P)
+                    nc.tensor.matmul_mx(
+                        out=acc[:],
+                        lhsT=d_codes[:, b_cols].bitcast(E5M2_X4),
+                        lhsT_scale=d_scales[:, b_cols],
+                        rhs=w_codes[:, n, :].bitcast(E4M3_X4),
+                        rhs_scale=w_scales[:, n, :],
+                        start=(h == 0 and product == 0 and nq == 0),
+                        stop=(h == 1 and product == 1 and nq == HALF_N - 1),
+                    )
+            if h == 1:
+                out_rows = work.tile([P, IN_C], F32, name="out_rows")
+                nc.scalar.copy(out=out_rows[:], in_=acc[:])
+                nc.scalar.dma_start(out=out[j * P : (j + 1) * P, :], in_=out_rows[:])
+
+        front(0)
+        front(1)
+        middle(0)
+        middle(1)
+        for a in range(N_PAIRS):
+            prepare_wim(a)
+        back(0)
+        back(1)
+
+        front(2)
+        for s in range(2, STAGES):
+            if s + 1 < STAGES:
+                front(s + 1)
+            middle(s)
+            if s - 1 >= 2:
+                back(s - 1)
+        back(STAGES - 1)

@@ -53,23 +53,20 @@ def tile_tensormoe_pa_v_kernel(tc, x, W_im, W_in, leak_m, leak_n, z_m, z_n, grad
         win_codes = weights.tile([P, HN, IN_C], U32, align_bytes=64)
         win_scales = weights.tile([P, HN, IN_C], U8, align_bytes=64)
 
-        def load_rows(j):
+        zns, gs, zms = {}, {}, {}
+
+        def load_zn_and_g(j):
             rows = slice(j * P, (j + 1) * P)
-            zn_halves = []
-            for u in range(2):
-                zn = loads.tile([P, HM // 2 * HN], F32, tag="z", bufs=6, name="zn")
-                m_range = slice(u * (HM // 2), (u + 1) * (HM // 2))
-                nc.sync.dma_start(out=zn[:], in_=z_n[rows, m_range, :].rearrange("b m n -> b (m n)"))
-                zn_halves.append(zn)
-            g = loads.tile([P, HN * HM], BF16, name="g")
-            nc.sync.dma_start(out=g[:], in_=grad_out[rows].rearrange("b n m -> b (n m)"))
-            zm_halves = []
-            for h in range(2):
-                zm = loads.tile([P, HALF_N * HM], F32, tag="z", bufs=6, name="zm")
-                n_range = slice(h * HALF_N, (h + 1) * HALF_N)
-                nc.sync.dma_start(out=zm[:], in_=z_m[rows, n_range, :].rearrange("b n m -> b (n m)"))
-                zm_halves.append(zm)
-            return zn_halves, g, zm_halves
+            zns[j] = loads.tile([P, HM * HN], F32, name="zn")
+            nc.sync.dma_start(out=zns[j][:], in_=z_n[rows].rearrange("b m n -> b (m n)"))
+            gs[j] = loads.tile([P, HN * HM], BF16, name="g")
+            nc.sync.dma_start(out=gs[j][:], in_=grad_out[rows].rearrange("b n m -> b (n m)"))
+
+        def load_zm(s):
+            j, h = divmod(s, 2)
+            zms[s] = loads.tile([P, HALF_N * HM], F32, name="zm")
+            n_range = slice(h * HALF_N, (h + 1) * HALF_N)
+            nc.sync.dma_start(out=zms[s][:], in_=z_m[j * P : (j + 1) * P, n_range, :].rearrange("b n m -> b (n m)"))
 
         win_rows = W_in.rearrange("(u q e) i n -> u q e (i n)", u=2, e=2)
         win_raws = []
@@ -81,7 +78,9 @@ def tile_tensormoe_pa_v_kernel(tc, x, W_im, W_in, leak_m, leak_n, z_m, z_n, grad
                     in_=win_rows[u, :, :, c * I_CHUNK * HN : (c + 1) * I_CHUNK * HN],
                 )
             win_raws.append(win_raw)
-        loaded = {0: load_rows(0)}
+        load_zn_and_g(0)
+        load_zm(0)
+        load_zm(1)
 
         def regroup_win(c):
             win_grouped = wstage.tile([P, HN, I_CHUNK, PACK], BF16, tag="grouped", bufs=3, name="win_grouped", align_bytes=64)
@@ -131,12 +130,10 @@ def tile_tensormoe_pa_v_kernel(tc, x, W_im, W_in, leak_m, leak_n, z_m, z_n, grad
                             in_=wim_words[:, 2 * i_half + cc, u * P : (u + 1) * P],
                             identity=ident[:],
                         )
-                dst = grouped_words[:, i_half * 2 * P : (i_half + 1) * 2 * P, :]
-                src = bank[:].rearrange("q u i -> q i u")
-                if i_half % 2 == 0:
-                    nc.scalar.copy(out=dst, in_=src)
-                else:
-                    nc.vector.tensor_copy(out=dst, in_=src)
+                nc.scalar.copy(
+                    out=grouped_words[:, i_half * 2 * P : (i_half + 1) * 2 * P, :],
+                    in_=bank[:].rearrange("q u i -> q i u"),
+                )
             nc.vector.quantize_mx(
                 out=wim_codes[:, 2 * a : 2 * a + 2, :].rearrange("q n i -> q (n i)").bitcast(E4M3_X4),
                 scales=wim_scales[:, 2 * a : 2 * a + 2, :].rearrange("q n i -> q (n i)"),
@@ -159,22 +156,19 @@ def tile_tensormoe_pa_v_kernel(tc, x, W_im, W_in, leak_m, leak_n, z_m, z_n, grad
 
         def front(s):
             j, h = divmod(s, 2)
-            zn_halves, g, zm_halves = loaded[j]
             if h == 0:
                 pos_n = work.tile([P, HN, HM], BF16, name="pos_n")
-                for u in range(2):
-                    m_range = slice(u * (HM // 2), (u + 1) * (HM // 2))
-                    nc.vector.tensor_single_scalar(
-                        out=pos_n[:, :, m_range].rearrange("b (hh nq) m -> b hh m nq", hh=2),
-                        in_=zn_halves[u][:].rearrange("b (m hh nq) -> b hh m nq", hh=2, nq=HALF_N),
-                        scalar=0.0,
-                        op=ALU.is_ge,
-                    )
+                nc.vector.tensor_single_scalar(
+                    out=pos_n[:].rearrange("b (hh nq) m -> b hh m nq", hh=2),
+                    in_=zns[j][:].rearrange("b (m hh nq) -> b hh m nq", hh=2, nq=HALF_N),
+                    scalar=0.0,
+                    op=ALU.is_ge,
+                )
                 pos_ns[j] = pos_n
             pos_m = work.tile([P, HALF_N * HM], BF16, name="pos_m")
-            nc.vector.tensor_single_scalar(out=pos_m[:], in_=zm_halves[h][:], scalar=0.0, op=ALU.is_ge)
+            nc.vector.tensor_single_scalar(out=pos_m[:], in_=zms[s][:], scalar=0.0, op=ALU.is_ge)
 
-            g_words = g[:].bitcast(F32)
+            g_words = gs[j][:].bitcast(F32)
             pos_n_words = pos_ns[j][:].rearrange("b n m -> b (n m)").bitcast(F32)
             pos_m_words = pos_m[:].bitcast(F32)
 
@@ -226,7 +220,9 @@ def tile_tensormoe_pa_v_kernel(tc, x, W_im, W_in, leak_m, leak_n, z_m, z_n, grad
                     )
             fronts[s] = (gT, fnT, fmT)
             if h == 0 and j + 1 < B_TILES:
-                loaded[j + 1] = load_rows(j + 1)
+                load_zn_and_g(j + 1)
+            if s + 2 < STAGES:
+                load_zm(s + 2)
 
         def middle(s):
             gT, fnT, fmT = fronts[s]

@@ -185,7 +185,7 @@ def tile_tensormoe_pa_v_kernel(tc, x, W_im, W_in, leak_m, leak_n, z_m, z_n, grad
                         for u in range(2):
                             words = slice(n * 2 * P + u * P, n * 2 * P + (u + 1) * P)
                             nc.tensor.transpose(out=bank[:, nn, u, :], in_=words_of[:, words], identity=ident[:])
-                nc.scalar.copy(
+                nc.vector.tensor_copy(
                     out=gT_words[:, 2 * pair : 2 * pair + 2],
                     in_=g_bank[:].rearrange("q nn u b -> q nn b u"),
                 )

@@ -140,16 +140,12 @@ def tile_tensormoe_pa_v_kernel(tc, x, W_im, W_in, leak_m, leak_n, z_m, z_n, grad
                 in_=wim_grouped[:],
             )
 
-        lm = const.tile([P, PACK], F32)
-        one_minus_lm = const.tile([P, PACK], F32)
-        ln = const.tile([P, HN], F32)
-        one_minus_ln = const.tile([P, HN], F32)
-        nc.vector.tensor_copy(out=lm[:], in_=lm_bf[:])
-        nc.vector.tensor_copy(out=ln[:], in_=ln_bf[:])
-        nc.vector.tensor_scalar(out=one_minus_lm[:], in0=lm[:], scalar1=-1.0, scalar2=1.0, op0=ALU.mult, op1=ALU.add)
-        nc.vector.tensor_scalar(out=one_minus_ln[:], in0=ln[:], scalar1=-1.0, scalar2=1.0, op0=ALU.mult, op1=ALU.add)
+        lm_minus_1 = const.tile([P, PACK], F32)
+        ln_minus_1 = const.tile([P, HN], F32)
+        nc.vector.tensor_scalar_add(out=lm_minus_1[:], in0=lm_bf[:], scalar1=-1.0)
+        nc.vector.tensor_scalar_add(out=ln_minus_1[:], in0=ln_bf[:], scalar1=-1.0)
 
-        pos_ns = {}
+        neg_ns = {}
         fronts = {}
         codes = {}
         acc_of = {}
@@ -157,20 +153,20 @@ def tile_tensormoe_pa_v_kernel(tc, x, W_im, W_in, leak_m, leak_n, z_m, z_n, grad
         def front(s):
             j, h = divmod(s, 2)
             if h == 0:
-                pos_n = work.tile([P, HN, HM], BF16, name="pos_n")
+                neg_n = work.tile([P, HN, HM], BF16, name="neg_n")
                 nc.vector.tensor_single_scalar(
-                    out=pos_n[:].rearrange("b (hh nq) m -> b hh m nq", hh=2),
+                    out=neg_n[:].rearrange("b (hh nq) m -> b hh m nq", hh=2),
                     in_=zns[j][:].rearrange("b (m hh nq) -> b hh m nq", hh=2, nq=HALF_N),
                     scalar=0.0,
-                    op=ALU.is_ge,
+                    op=ALU.is_lt,
                 )
-                pos_ns[j] = pos_n
-            pos_m = work.tile([P, HALF_N * HM], BF16, name="pos_m")
-            nc.vector.tensor_single_scalar(out=pos_m[:], in_=zms[s][:], scalar=0.0, op=ALU.is_ge)
+                neg_ns[j] = neg_n
+            neg_m = work.tile([P, HALF_N * HM], BF16, name="neg_m")
+            nc.vector.tensor_single_scalar(out=neg_m[:], in_=zms[s][:], scalar=0.0, op=ALU.is_lt)
 
             g_words = gs[j][:].bitcast(F32)
-            pos_n_words = pos_ns[j][:].rearrange("b n m -> b (n m)").bitcast(F32)
-            pos_m_words = pos_m[:].bitcast(F32)
+            neg_n_words = neg_ns[j][:].rearrange("b n m -> b (n m)").bitcast(F32)
+            neg_m_words = neg_m[:].bitcast(F32)
 
             gT = work.tile([P, STAGE * PACK], BF16, name="gT")
             gT_words = gT[:].bitcast(F32).rearrange("q (nq b u) -> q nq b u", nq=HALF_N, u=2)
@@ -179,13 +175,13 @@ def tile_tensormoe_pa_v_kernel(tc, x, W_im, W_in, leak_m, leak_n, z_m, z_n, grad
             for pair in range(HALF_N // 2):
                 g_bank = tpsum.tile([P, 2, 2, P], F32, tag="bank", name="g_bank")
                 n_bank = tpsum.tile([P, 2, 2, P], F32, tag="bank", name="n_bank")
-                for bank, words_of in ((g_bank, g_words), (n_bank, pos_n_words)):
+                for bank, words_of in ((g_bank, g_words), (n_bank, neg_n_words)):
                     for nn in range(2):
                         n = h * HALF_N + 2 * pair + nn
                         for u in range(2):
                             words = slice(n * 2 * P + u * P, n * 2 * P + (u + 1) * P)
                             nc.tensor.transpose(out=bank[:, nn, u, :], in_=words_of[:, words], identity=ident[:])
-                nc.vector.tensor_copy(
+                nc.scalar.copy(
                     out=gT_words[:, 2 * pair : 2 * pair + 2],
                     in_=g_bank[:].rearrange("q nn u b -> q nn b u"),
                 )
@@ -197,9 +193,9 @@ def tile_tensormoe_pa_v_kernel(tc, x, W_im, W_in, leak_m, leak_n, z_m, z_n, grad
                     nc.scalar.activation(
                         out=fnT_view[:, 2 * pair + nn],
                         in_=n_bank_bf[:, nn],
-                        func=ACT.Identity,
-                        scale=one_minus_ln[:, n : n + 1],
-                        bias=ln[:, n : n + 1],
+                        func=ACT.Copy,
+                        scale=ln_minus_1[:, n : n + 1],
+                        bias=1.0,
                     )
 
             fmT = work.tile([P, PACK, STAGE], BF16, name="fmT")
@@ -207,16 +203,16 @@ def tile_tensormoe_pa_v_kernel(tc, x, W_im, W_in, leak_m, leak_n, z_m, z_n, grad
                 m_bank = tpsum.tile([P, HALF_N, P], F32, tag="bank", name="m_bank")
                 for nq in range(HALF_N):
                     words = slice(nq * 2 * P + u * P, nq * 2 * P + (u + 1) * P)
-                    nc.tensor.transpose(out=m_bank[:, nq, :], in_=pos_m_words[:, words], identity=ident[:])
+                    nc.tensor.transpose(out=m_bank[:, nq, :], in_=neg_m_words[:, words], identity=ident[:])
                 m_bank_bf = m_bank[:].rearrange("q nq b -> q (nq b)").bitcast(BF16).rearrange("q (x e) -> q x e", e=2)
                 for e in range(2):
                     t = 2 * u + e
                     nc.scalar.activation(
                         out=fmT[:, t, :],
                         in_=m_bank_bf[:, :, e],
-                        func=ACT.Identity,
-                        scale=one_minus_lm[:, t : t + 1],
-                        bias=lm[:, t : t + 1],
+                        func=ACT.Copy,
+                        scale=lm_minus_1[:, t : t + 1],
+                        bias=1.0,
                     )
             fronts[s] = (gT, fnT, fmT)
             if h == 0 and j + 1 < B_TILES:

@@ -33,7 +33,8 @@ def tile_tensormoe_pa_v_kernel(tc, x, W_im, W_in, leak_m, leak_n, z_m, z_n, grad
         tc.tile_pool(name="wstage", bufs=2) as wstage,
         tc.tile_pool(name="loads", bufs=2) as loads,
         tc.tile_pool(name="work", bufs=2) as work,
-        tc.psum_pool(name="tpsum", bufs=6) as tpsum,
+        tc.psum_pool(name="tpsum", bufs=4) as tpsum,
+        tc.psum_pool(name="gpsum", bufs=2) as gpsum,
         tc.psum_pool(name="accs", bufs=2) as accs,
         tc.manual_schedule(),
     ):
@@ -150,6 +151,8 @@ def tile_tensormoe_pa_v_kernel(tc, x, W_im, W_in, leak_m, leak_n, z_m, z_n, grad
         codes = {}
         acc_of = {}
 
+        g_banks = {}
+
         def front(s):
             j, h = divmod(s, 2)
             if h == 0:
@@ -164,27 +167,18 @@ def tile_tensormoe_pa_v_kernel(tc, x, W_im, W_in, leak_m, leak_n, z_m, z_n, grad
             neg_m = work.tile([P, HALF_N * HM], BF16, name="neg_m")
             nc.vector.tensor_single_scalar(out=neg_m[:], in_=zms[s][:], scalar=0.0, op=ALU.is_lt)
 
-            g_words = gs[j][:].bitcast(F32)
             neg_n_words = neg_ns[j][:].rearrange("b n m -> b (n m)").bitcast(F32)
             neg_m_words = neg_m[:].bitcast(F32)
 
-            gT = work.tile([P, STAGE * PACK], BF16, name="gT")
-            gT_words = gT[:].bitcast(F32).rearrange("q (nq b u) -> q nq b u", nq=HALF_N, u=2)
             fnT = work.tile([P, STAGE * PACK], BF16, name="fnT")
             fnT_view = fnT[:].rearrange("q (nq b u e) -> q nq b u e", nq=HALF_N, u=2, e=2)
             for pair in range(HALF_N // 2):
-                g_bank = tpsum.tile([P, 2, 2, P], F32, tag="bank", name="g_bank")
                 n_bank = tpsum.tile([P, 2, 2, P], F32, tag="bank", name="n_bank")
-                for bank, words_of in ((g_bank, g_words), (n_bank, neg_n_words)):
-                    for nn in range(2):
-                        n = h * HALF_N + 2 * pair + nn
-                        for u in range(2):
-                            words = slice(n * 2 * P + u * P, n * 2 * P + (u + 1) * P)
-                            nc.tensor.transpose(out=bank[:, nn, u, :], in_=words_of[:, words], identity=ident[:])
-                nc.scalar.copy(
-                    out=gT_words[:, 2 * pair : 2 * pair + 2],
-                    in_=g_bank[:].rearrange("q nn u b -> q nn b u"),
-                )
+                for nn in range(2):
+                    n = h * HALF_N + 2 * pair + nn
+                    for u in range(2):
+                        words = slice(n * 2 * P + u * P, n * 2 * P + (u + 1) * P)
+                        nc.tensor.transpose(out=n_bank[:, nn, u, :], in_=neg_n_words[:, words], identity=ident[:])
                 n_bank_bf = n_bank[:].rearrange("q nn u b -> q (nn u b)").bitcast(BF16).rearrange(
                     "q (nn u b e) -> q nn b u e", nn=2, u=2, e=2
                 )
@@ -214,23 +208,38 @@ def tile_tensormoe_pa_v_kernel(tc, x, W_im, W_in, leak_m, leak_n, z_m, z_n, grad
                         scale=lm_minus_1[:, t : t + 1],
                         bias=1.0,
                     )
-            fronts[s] = (gT, fnT, fmT)
+            fronts[s] = (fnT, fmT)
             if h == 0 and j + 1 < B_TILES:
                 load_zn_and_g(j + 1)
             if s + 2 < STAGES:
                 load_zm(s + 2)
 
+        def transpose_g(s):
+            j, h = divmod(s, 2)
+            g_words = gs[j][:].bitcast(F32)
+            g_banks[s] = []
+            for pair in range(HALF_N // 2):
+                g_bank = gpsum.tile([P, 2, 2 * P], F32, name="g_bank")
+                for nn in range(2):
+                    n = h * HALF_N + 2 * pair + nn
+                    for u in range(2):
+                        words = slice(n * 2 * P + u * P, n * 2 * P + (u + 1) * P)
+                        nc.tensor.transpose(out=g_bank[:, u, nn * P : (nn + 1) * P], in_=g_words[:, words], identity=ident[:])
+                g_banks[s].append(g_bank)
+
         def middle(s):
-            gT, fnT, fmT = fronts[s]
+            fnT, fmT = fronts[s]
             dnT = work.tile([P, STAGE * PACK], BF16, name="dnT", bufs=1, align_bytes=64)
             dmT = work.tile([P, STAGE * PACK], BF16, name="dmT", bufs=1, align_bytes=64)
-            nc.vector.tensor_tensor(out=dnT[:], in0=fnT[:], in1=gT[:], op=ALU.mult)
-            nc.vector.tensor_tensor(
-                out=dmT[:].rearrange("q (x t) -> q x t", t=PACK),
-                in0=fmT[:].rearrange("q t x -> q x t"),
-                in1=gT[:].rearrange("q (x t) -> q x t", t=PACK),
-                op=ALU.mult,
-            )
+            dnT_view = dnT[:].rearrange("q (x u e) -> q x u e", u=2, e=2)
+            dmT_view = dmT[:].rearrange("q (x u e) -> q x u e", u=2, e=2)
+            fnT_view = fnT[:].rearrange("q (x u e) -> q x u e", u=2, e=2)
+            fmT_view = fmT[:].rearrange("q (u e) x -> q x u e", u=2)
+            for pair in range(HALF_N // 2):
+                two = slice(2 * P * pair, 2 * P * (pair + 1))
+                g_view = g_banks[s][pair][:].rearrange("q u x -> q (u x)").bitcast(BF16).rearrange("q (u x e) -> q x u e", u=2, e=2)
+                nc.vector.tensor_tensor(out=dnT_view[:, two], in0=fnT_view[:, two], in1=g_view, op=ALU.mult)
+                nc.vector.tensor_tensor(out=dmT_view[:, two], in0=fmT_view[:, two], in1=g_view, op=ALU.mult)
             dn_codes = work.tile([P, STAGE], U32, name="dn_codes", align_bytes=64)
             dn_scales = work.tile([P, STAGE], U8, name="dn_scales", align_bytes=64)
             dm_codes = work.tile([P, STAGE], U32, name="dm_codes", align_bytes=64)
@@ -264,8 +273,10 @@ def tile_tensormoe_pa_v_kernel(tc, x, W_im, W_in, leak_m, leak_n, z_m, z_n, grad
                 nc.scalar.dma_start(out=out[j * P : (j + 1) * P, :], in_=out_rows[:])
 
         front(0)
+        transpose_g(0)
         front(1)
         middle(0)
+        transpose_g(1)
         middle(1)
         for a in range(N_PAIRS):
             prepare_wim(a)
@@ -273,10 +284,13 @@ def tile_tensormoe_pa_v_kernel(tc, x, W_im, W_in, leak_m, leak_n, z_m, z_n, grad
         back(1)
 
         front(2)
+        transpose_g(2)
         for s in range(2, STAGES):
             if s + 1 < STAGES:
                 front(s + 1)
             middle(s)
             if s - 1 >= 2:
                 back(s - 1)
+            if s + 1 < STAGES:
+                transpose_g(s + 1)
         back(STAGES - 1)

@@ -192,7 +192,7 @@ def tile_tensormoe_pa_v_kernel(tc, x, W_im, W_in, leak_m, leak_n, z_m, z_n, grad
                         bias=1.0,
                     )
 
-            fmT = work.tile([P, PACK, STAGE], BF16, name="fmT")
+            fmT = work.tile([P, 2, STAGE, 2], BF16, name="fmT")
             for u in range(2):
                 m_bank = tpsum.tile([P, HALF_N, P], F32, tag="bank", name="m_bank")
                 for nq in range(HALF_N):
@@ -202,7 +202,7 @@ def tile_tensormoe_pa_v_kernel(tc, x, W_im, W_in, leak_m, leak_n, z_m, z_n, grad
                 for e in range(2):
                     t = 2 * u + e
                     nc.scalar.activation(
-                        out=fmT[:, t, :],
+                        out=fmT[:, u, :, e],
                         in_=m_bank_bf[:, :, e],
                         func=ACT.Copy,
                         scale=lm_minus_1[:, t : t + 1],
@@ -234,7 +234,7 @@ def tile_tensormoe_pa_v_kernel(tc, x, W_im, W_in, leak_m, leak_n, z_m, z_n, grad
             dnT_view = dnT[:].rearrange("q (x u e) -> q x u e", u=2, e=2)
             dmT_view = dmT[:].rearrange("q (x u e) -> q x u e", u=2, e=2)
             fnT_view = fnT[:].rearrange("q (x u e) -> q x u e", u=2, e=2)
-            fmT_view = fmT[:].rearrange("q (u e) x -> q x u e", u=2)
+            fmT_view = fmT[:].rearrange("q u x e -> q x u e")
             for pair in range(HALF_N // 2):
                 two = slice(2 * P * pair, 2 * P * (pair + 1))
                 g_view = g_banks[s][pair][:].rearrange("q u x -> q (u x)").bitcast(BF16).rearrange("q (u x e) -> q x u e", u=2, e=2)

@@ -39,6 +39,8 @@ def tile_tensormoe_pa_v_kernel(tc, x, W_im, W_in, leak_m, leak_n, z_m, z_n, grad
         tc.manual_schedule(),
     ):
 
+        ident = const.tile([P, P], F32)
+        make_identity(nc, ident[:])
         lm_bf = const.tile([P, PACK], BF16)
         nc.gpsimd.dma_start(
             out=lm_bf[:].rearrange("q (u e) -> q u e", u=2),
@@ -46,15 +48,34 @@ def tile_tensormoe_pa_v_kernel(tc, x, W_im, W_in, leak_m, leak_n, z_m, z_n, grad
         )
         ln_bf = const.tile([P, HN], BF16)
         nc.gpsimd.dma_start(out=ln_bf[:], in_=leak_n.partition_broadcast(P))
-        ident = const.tile([P, P], F32)
-        make_identity(nc, ident[:])
+        zero = const.tile([P, 1], F32)
+        warm = const.tile([P, 1], F32)
+        nc.vector.memset(zero[:], 0.0)
+        nc.scalar.copy(out=warm[:], in_=zero[:])
 
         wim_codes = weights.tile([P, HN, IN_C], U32, align_bytes=64)
         wim_scales = weights.tile([P, HN, IN_C], U8, align_bytes=64)
         win_codes = weights.tile([P, HN, IN_C], U32, align_bytes=64)
         win_scales = weights.tile([P, HN, IN_C], U8, align_bytes=64)
 
-        zns, gs, zms = {}, {}, {}
+        zns, gs = {}, {}
+        zms = {}
+        win_raws, wim_raws = {}, {}
+        win_rows = W_in.rearrange("(u q e) i n -> u q e (i n)", u=2, e=2)
+
+        def load_win(c):
+            win_raw = wstage.tile([P, PACK, I_CHUNK, HN], BF16, tag="raw", bufs=4, name="win_raw")
+            for u in range(2):
+                nc.sync.dma_start(
+                    out=win_raw[:, 2 * u : 2 * u + 2].rearrange("q e i n -> q e (i n)"),
+                    in_=win_rows[u, :, :, c * I_CHUNK * HN : (c + 1) * I_CHUNK * HN],
+                )
+            win_raws[c] = win_raw
+
+        def load_wim(a):
+            wim_raw = wstage.tile([P, 2 * IN_C // P, HM], BF16, tag="raw", bufs=4, name="wim_raw")
+            nc.sync.dma_start(out=wim_raw[:], in_=W_im[2 * a : 2 * a + 2].rearrange("n (c p) m -> p (n c) m", p=P))
+            wim_raws[a] = wim_raw
 
         def load_zn_and_g(j):
             rows = slice(j * P, (j + 1) * P)
@@ -65,23 +86,17 @@ def tile_tensormoe_pa_v_kernel(tc, x, W_im, W_in, leak_m, leak_n, z_m, z_n, grad
 
         def load_zm(s):
             j, h = divmod(s, 2)
-            zms[s] = loads.tile([P, HALF_N * HM], F32, name="zm")
+            zms[s] = loads.tile([P, HALF_N * HM], F32, name="zm", bufs=3)
             n_range = slice(h * HALF_N, (h + 1) * HALF_N)
             nc.sync.dma_start(out=zms[s][:], in_=z_m[j * P : (j + 1) * P, n_range, :].rearrange("b n m -> b (n m)"))
 
-        win_rows = W_in.rearrange("(u q e) i n -> u q e (i n)", u=2, e=2)
-        win_raws = []
-        for c in range(I_CHUNKS):
-            win_raw = wstage.tile([P, PACK, I_CHUNK, HN], BF16, tag="raw", bufs=4, name="win_raw")
-            for u in range(2):
-                nc.sync.dma_start(
-                    out=win_raw[:, 2 * u : 2 * u + 2].rearrange("q e i n -> q e (i n)"),
-                    in_=win_rows[u, :, :, c * I_CHUNK * HN : (c + 1) * I_CHUNK * HN],
-                )
-            win_raws.append(win_raw)
-        load_zn_and_g(0)
-        load_zm(0)
-        load_zm(1)
+        def load_behind(s):
+            if s % 2 == 1 and (s + 3) // 2 < B_TILES:
+                load_zn_and_g((s + 3) // 2)
+            if s + 3 < STAGES:
+                load_zm(s + 3)
+
+        win_groupeds = {}
 
         def regroup_win(c):
             win_grouped = wstage.tile([P, HN, I_CHUNK, PACK], BF16, tag="grouped", bufs=3, name="win_grouped", align_bytes=64)
@@ -93,32 +108,20 @@ def tile_tensormoe_pa_v_kernel(tc, x, W_im, W_in, leak_m, leak_n, z_m, z_n, grad
                     nc.vector.tensor_copy(out=dst, in_=src)
                 else:
                     nc.scalar.copy(out=dst, in_=src)
-            return win_grouped
+            win_groupeds[c] = win_grouped
 
-        def quantise_win(c, win_grouped):
+        def quantise_win(c):
             i_cols = slice(c * I_CHUNK, (c + 1) * I_CHUNK)
             for n in range(HN):
                 nc.vector.quantize_mx(
                     out=win_codes[:, n, i_cols].bitcast(E4M3_X4),
                     scales=win_scales[:, n, i_cols],
-                    in_=win_grouped[:, n].rearrange("q i t -> q (i t)"),
+                    in_=win_groupeds[c][:, n].rearrange("q i t -> q (i t)"),
                 )
 
-        from_scalar = {}
-        for c in range(0, I_CHUNKS, 2):
-            from_vector = regroup_win(c)
-            from_scalar[c + 1] = regroup_win(c + 1)
-            quantise_win(c, from_vector)
-        for c in range(1, I_CHUNKS, 2):
-            quantise_win(c, from_scalar[c])
+        wim_groupeds = {}
 
-        wim_raws = []
-        for a in range(N_PAIRS):
-            wim_raw = wstage.tile([P, 2 * IN_C // P, HM], BF16, tag="raw", bufs=4, name="wim_raw")
-            nc.sync.dma_start(out=wim_raw[:], in_=W_im[2 * a : 2 * a + 2].rearrange("n (c p) m -> p (n c) m", p=P))
-            wim_raws.append(wim_raw)
-
-        def prepare_wim(a):
+        def regroup_wim(a):
             wim_words = wim_raws[a][:].rearrange("p c m -> p (c m)").bitcast(F32).rearrange("p (c w) -> p c w", w=HM // 2)
             wim_grouped = wstage.tile([P, 2 * IN_C * PACK], BF16, tag="grouped", bufs=3, name="wim_grouped", align_bytes=64)
             grouped_words = wim_grouped[:].bitcast(F32).rearrange("q (i u) -> q i u", u=2)
@@ -135,50 +138,47 @@ def tile_tensormoe_pa_v_kernel(tc, x, W_im, W_in, leak_m, leak_n, z_m, z_n, grad
                     out=grouped_words[:, i_half * 2 * P : (i_half + 1) * 2 * P, :],
                     in_=bank[:].rearrange("q u i -> q i u"),
                 )
+            wim_groupeds[a] = wim_grouped
+
+        def quantise_wim(a):
             nc.vector.quantize_mx(
                 out=wim_codes[:, 2 * a : 2 * a + 2, :].rearrange("q n i -> q (n i)").bitcast(E4M3_X4),
                 scales=wim_scales[:, 2 * a : 2 * a + 2, :].rearrange("q n i -> q (n i)"),
-                in_=wim_grouped[:],
+                in_=wim_groupeds[a][:],
             )
 
         lm_minus_1 = const.tile([P, PACK], F32)
         ln_minus_1 = const.tile([P, HN], F32)
-        nc.vector.tensor_scalar_add(out=lm_minus_1[:], in0=lm_bf[:], scalar1=-1.0)
-        nc.vector.tensor_scalar_add(out=ln_minus_1[:], in0=ln_bf[:], scalar1=-1.0)
 
-        neg_ns = {}
-        fronts = {}
-        codes = {}
+        neg_ns, neg_ms, fns, fms, g_banks, products, codes = {}, {}, {}, {}, {}, {}, {}
         acc_of = {}
 
-        g_banks = {}
-
-        def front(s):
+        def signs_n(s):
             j, h = divmod(s, 2)
-            if h == 0:
-                neg_n = work.tile([P, HN, HM], BF16, name="neg_n")
-                nc.vector.tensor_single_scalar(
-                    out=neg_n[:].rearrange("b (hh nq) m -> b hh m nq", hh=2),
-                    in_=zns[j][:].rearrange("b (m hh nq) -> b hh m nq", hh=2, nq=HALF_N),
-                    scalar=0.0,
-                    op=ALU.is_lt,
-                )
-                neg_ns[j] = neg_n
-            neg_m = work.tile([P, HALF_N * HM], BF16, name="neg_m")
-            nc.vector.tensor_single_scalar(out=neg_m[:], in_=zms[s][:], scalar=0.0, op=ALU.is_lt)
+            neg_ns[s] = work.tile([P, HALF_N, HM], BF16, name="neg_n")
+            nc.vector.tensor_single_scalar(
+                out=neg_ns[s][:].rearrange("b nq m -> b m nq"),
+                in_=zns[j][:].rearrange("b (m hh nq) -> b hh m nq", hh=2, nq=HALF_N)[:, h],
+                scalar=0.0,
+                op=ALU.is_lt,
+            )
 
-            neg_n_words = neg_ns[j][:].rearrange("b n m -> b (n m)").bitcast(F32)
-            neg_m_words = neg_m[:].bitcast(F32)
+        def signs_m(s):
+            neg_ms[s] = work.tile([P, HALF_N * HM], BF16, name="neg_m")
+            nc.vector.tensor_single_scalar(out=neg_ms[s][:], in_=zms[s][:], scalar=0.0, op=ALU.is_lt)
 
-            fnT = work.tile([P, STAGE * PACK], BF16, name="fnT")
-            fnT_view = fnT[:].rearrange("q (nq b u e) -> q nq b u e", nq=HALF_N, u=2, e=2)
+        def factors_n(s):
+            h = s % 2
+            words_of = neg_ns[s][:].rearrange("b nq m -> b (nq m)").bitcast(F32)
+            fns[s] = work.tile([P, STAGE * PACK], BF16, name="fnT")
+            fnT_view = fns[s][:].rearrange("q (nq b u e) -> q nq b u e", nq=HALF_N, u=2, e=2)
             for pair in range(HALF_N // 2):
                 n_bank = tpsum.tile([P, 2, 2, P], F32, tag="bank", name="n_bank")
                 for nn in range(2):
-                    n = h * HALF_N + 2 * pair + nn
+                    nq = 2 * pair + nn
                     for u in range(2):
-                        words = slice(n * 2 * P + u * P, n * 2 * P + (u + 1) * P)
-                        nc.tensor.transpose(out=n_bank[:, nn, u, :], in_=neg_n_words[:, words], identity=ident[:])
+                        words = slice(nq * 2 * P + u * P, nq * 2 * P + (u + 1) * P)
+                        nc.tensor.transpose(out=n_bank[:, nn, u, :], in_=words_of[:, words], identity=ident[:])
                 n_bank_bf = n_bank[:].rearrange("q nn u b -> q (nn u b)").bitcast(BF16).rearrange(
                     "q (nn u b e) -> q nn b u e", nn=2, u=2, e=2
                 )
@@ -192,27 +192,24 @@ def tile_tensormoe_pa_v_kernel(tc, x, W_im, W_in, leak_m, leak_n, z_m, z_n, grad
                         bias=1.0,
                     )
 
-            fmT = work.tile([P, 2, STAGE, 2], BF16, name="fmT")
+        def factors_m(s):
+            words_of = neg_ms[s][:].bitcast(F32)
+            fms[s] = work.tile([P, 2, STAGE, 2], BF16, name="fmT")
             for u in range(2):
                 m_bank = tpsum.tile([P, HALF_N, P], F32, tag="bank", name="m_bank")
                 for nq in range(HALF_N):
                     words = slice(nq * 2 * P + u * P, nq * 2 * P + (u + 1) * P)
-                    nc.tensor.transpose(out=m_bank[:, nq, :], in_=neg_m_words[:, words], identity=ident[:])
+                    nc.tensor.transpose(out=m_bank[:, nq, :], in_=words_of[:, words], identity=ident[:])
                 m_bank_bf = m_bank[:].rearrange("q nq b -> q (nq b)").bitcast(BF16).rearrange("q (x e) -> q x e", e=2)
                 for e in range(2):
                     t = 2 * u + e
                     nc.scalar.activation(
-                        out=fmT[:, u, :, e],
+                        out=fms[s][:, u, :, e],
                         in_=m_bank_bf[:, :, e],
                         func=ACT.Copy,
                         scale=lm_minus_1[:, t : t + 1],
                         bias=1.0,
                     )
-            fronts[s] = (fnT, fmT)
-            if h == 0 and j + 1 < B_TILES:
-                load_zn_and_g(j + 1)
-            if s + 2 < STAGES:
-                load_zm(s + 2)
 
         def transpose_g(s):
             j, h = divmod(s, 2)
@@ -227,19 +224,28 @@ def tile_tensormoe_pa_v_kernel(tc, x, W_im, W_in, leak_m, leak_n, z_m, z_n, grad
                         nc.tensor.transpose(out=g_bank[:, u, nn * P : (nn + 1) * P], in_=g_words[:, words], identity=ident[:])
                 g_banks[s].append(g_bank)
 
-        def middle(s):
-            fnT, fmT = fronts[s]
-            dnT = work.tile([P, STAGE * PACK], BF16, name="dnT", bufs=1, align_bytes=64)
-            dmT = work.tile([P, STAGE * PACK], BF16, name="dmT", bufs=1, align_bytes=64)
-            dnT_view = dnT[:].rearrange("q (x u e) -> q x u e", u=2, e=2)
-            dmT_view = dmT[:].rearrange("q (x u e) -> q x u e", u=2, e=2)
-            fnT_view = fnT[:].rearrange("q (x u e) -> q x u e", u=2, e=2)
-            fmT_view = fmT[:].rearrange("q u x e -> q x u e")
+        def pair_views(s, pair):
+            dnT, dmT = products[s]
+            two = slice(2 * P * pair, 2 * P * (pair + 1))
+            g_view = g_banks[s][pair][:].rearrange("q u x -> q (u x)").bitcast(BF16).rearrange("q (u x e) -> q x u e", u=2, e=2)
+            dn_view = dnT[:].rearrange("q (x u e) -> q x u e", u=2, e=2)[:, two]
+            dm_view = dmT[:].rearrange("q (x u e) -> q x u e", u=2, e=2)[:, two]
+            fn_view = fns[s][:].rearrange("q (x u e) -> q x u e", u=2, e=2)[:, two]
+            fm_view = fms[s][:].rearrange("q u x e -> q x u e")[:, two]
+            return g_view, dn_view, fn_view, dm_view, fm_view
+
+        def multiply(s):
+            products[s] = (
+                work.tile([P, STAGE * PACK], BF16, name="dnT", bufs=1, align_bytes=64),
+                work.tile([P, STAGE * PACK], BF16, name="dmT", bufs=1, align_bytes=64),
+            )
             for pair in range(HALF_N // 2):
-                two = slice(2 * P * pair, 2 * P * (pair + 1))
-                g_view = g_banks[s][pair][:].rearrange("q u x -> q (u x)").bitcast(BF16).rearrange("q (u x e) -> q x u e", u=2, e=2)
-                nc.vector.tensor_tensor(out=dnT_view[:, two], in0=fnT_view[:, two], in1=g_view, op=ALU.mult)
-                nc.vector.tensor_tensor(out=dmT_view[:, two], in0=fmT_view[:, two], in1=g_view, op=ALU.mult)
+                g_view, dn_view, fn_view, dm_view, fm_view = pair_views(s, pair)
+                nc.vector.tensor_tensor(out=dn_view, in0=fn_view, in1=g_view, op=ALU.mult)
+                nc.vector.tensor_tensor(out=dm_view, in0=fm_view, in1=g_view, op=ALU.mult)
+
+        def quantise(s):
+            dnT, dmT = products[s]
             dn_codes = work.tile([P, STAGE], U32, name="dn_codes", align_bytes=64)
             dn_scales = work.tile([P, STAGE], U8, name="dn_scales", align_bytes=64)
             dm_codes = work.tile([P, STAGE], U32, name="dm_codes", align_bytes=64)
@@ -248,7 +254,7 @@ def tile_tensormoe_pa_v_kernel(tc, x, W_im, W_in, leak_m, leak_n, z_m, z_n, grad
             nc.vector.quantize_mx(out=dm_codes[:].bitcast(E5M2_X4), scales=dm_scales[:], in_=dmT[:])
             codes[s] = ((dn_codes, dn_scales, win_codes, win_scales), (dm_codes, dm_scales, wim_codes, wim_scales))
 
-        def back(s):
+        def passes(s):
             j, h = divmod(s, 2)
             if h == 0:
                 acc_of[j] = accs.tile([P, IN_C], F32, name="acc")
@@ -272,25 +278,71 @@ def tile_tensormoe_pa_v_kernel(tc, x, W_im, W_in, leak_m, leak_n, z_m, z_n, grad
                 nc.scalar.copy(out=out_rows[:], in_=acc[:])
                 nc.scalar.dma_start(out=out[j * P : (j + 1) * P, :], in_=out_rows[:])
 
-        front(0)
+        for c in range(I_CHUNKS):
+            load_win(c)
+        regroup_win(0)
+        regroup_win(1)
+        load_wim(0)
+        load_zn_and_g(0)
+        load_wim(1)
+        load_zm(0)
+        quantise_win(0)
+        regroup_win(2)
+        load_wim(2)
+        load_zm(1)
+        quantise_win(2)
+        quantise_win(1)
+        regroup_win(3)
+        load_wim(3)
+        load_zn_and_g(1)
+        load_zm(2)
+        regroup_wim(0)
+        quantise_win(3)
+        nc.vector.tensor_scalar_add(out=lm_minus_1[:], in0=lm_bf[:], scalar1=-1.0)
+        nc.vector.tensor_scalar_add(out=ln_minus_1[:], in0=ln_bf[:], scalar1=-1.0)
+        signs_n(0)
+        factors_n(0)
         transpose_g(0)
-        front(1)
-        middle(0)
+        quantise_wim(0)
+        signs_n(1)
+        factors_n(1)
+        signs_m(0)
+        regroup_wim(1)
+        factors_m(0)
+        load_behind(0)
+        quantise_wim(1)
+        regroup_wim(2)
+        signs_m(1)
+        multiply(0)
         transpose_g(1)
-        middle(1)
-        for a in range(N_PAIRS):
-            prepare_wim(a)
-        back(0)
-        back(1)
-
-        front(2)
+        factors_m(1)
+        load_behind(1)
+        quantise(0)
+        quantise_wim(2)
+        regroup_wim(3)
+        passes(0)
+        multiply(1)
+        quantise(1)
+        signs_n(2)
+        factors_n(2)
+        quantise_wim(3)
+        signs_m(2)
+        factors_m(2)
+        passes(1)
         transpose_g(2)
+        load_behind(2)
+
         for s in range(2, STAGES):
             if s + 1 < STAGES:
-                front(s + 1)
-            middle(s)
+                signs_n(s + 1)
+                signs_m(s + 1)
+                factors_n(s + 1)
+                factors_m(s + 1)
+            multiply(s)
+            quantise(s)
             if s - 1 >= 2:
-                back(s - 1)
+                passes(s - 1)
             if s + 1 < STAGES:
                 transpose_g(s + 1)
-        back(STAGES - 1)
+                load_behind(s + 1)
+        passes(STAGES - 1)

@@ -41,17 +41,18 @@ def tile_tensormoe_pa_v_kernel(tc, x, W_im, W_in, leak_m, leak_n, z_m, z_n, grad
 
         ident = const.tile([P, P], F32)
         make_identity(nc, ident[:])
-        lm_bf = const.tile([P, PACK], BF16)
-        nc.gpsimd.dma_start(
-            out=lm_bf[:].rearrange("q (u e) -> q u e", u=2),
-            in_=leak_m.rearrange("(u q e) -> q u e", u=2, e=2),
-        )
-        ln_bf = const.tile([P, HN], BF16)
-        nc.gpsimd.dma_start(out=ln_bf[:], in_=leak_n.partition_broadcast(P))
         zero = const.tile([P, 1], F32)
         warm = const.tile([P, 1], F32)
         nc.vector.memset(zero[:], 0.0)
         nc.scalar.copy(out=warm[:], in_=zero[:])
+        lm_rows = const.tile([P, 2 * P], BF16)
+        ln_rows = const.tile([P, HN], BF16)
+        ones = const.tile([P, P], BF16)
+        nc.vector.memset(lm_rows[:], 0.0)
+        nc.vector.memset(ln_rows[:], 0.0)
+        nc.gpsimd.memset(ones[:], 1.0)
+        nc.scalar.dma_start(out=lm_rows[0:2, :], in_=leak_m.rearrange("(u w) -> u w", u=2))
+        nc.scalar.dma_start(out=ln_rows[0:1, :], in_=leak_n.unsqueeze(0))
 
         wim_codes = weights.tile([P, HN, IN_C], U32, align_bytes=64)
         wim_scales = weights.tile([P, HN, IN_C], U8, align_bytes=64)
@@ -74,13 +75,19 @@ def tile_tensormoe_pa_v_kernel(tc, x, W_im, W_in, leak_m, leak_n, z_m, z_n, grad
 
         def load_wim(a):
             wim_raw = wstage.tile([P, 2 * IN_C // P, HM], BF16, tag="raw", bufs=4, name="wim_raw")
-            nc.sync.dma_start(out=wim_raw[:], in_=W_im[2 * a : 2 * a + 2].rearrange("n (c p) m -> p (n c) m", p=P))
+            nc.sync.dma_start(
+                out=wim_raw[:].rearrange("p (n c) m -> p n c m", n=2),
+                in_=W_im[2 * a : 2 * a + 2].rearrange("n (p c) m -> p n c m", p=P),
+            )
             wim_raws[a] = wim_raw
 
-        def load_zn_and_g(j):
+        def load_zn(j):
             rows = slice(j * P, (j + 1) * P)
             zns[j] = loads.tile([P, HM * HN], F32, name="zn")
             nc.sync.dma_start(out=zns[j][:], in_=z_n[rows].rearrange("b m n -> b (m n)"))
+
+        def load_g(j):
+            rows = slice(j * P, (j + 1) * P)
             gs[j] = loads.tile([P, HN * HM], BF16, name="g")
             nc.sync.dma_start(out=gs[j][:], in_=grad_out[rows].rearrange("b n m -> b (n m)"))
 
@@ -92,40 +99,44 @@ def tile_tensormoe_pa_v_kernel(tc, x, W_im, W_in, leak_m, leak_n, z_m, z_n, grad
 
         def load_behind(s):
             if s % 2 == 1 and (s + 3) // 2 < B_TILES:
-                load_zn_and_g((s + 3) // 2)
+                load_zn((s + 3) // 2)
             if s + 3 < STAGES:
                 load_zm(s + 3)
+            if s % 2 == 1 and (s + 3) // 2 < B_TILES:
+                load_g((s + 3) // 2)
 
         win_groupeds = {}
 
-        def regroup_win(c):
-            win_grouped = wstage.tile([P, HN, I_CHUNK, PACK], BF16, tag="grouped", bufs=3, name="win_grouped", align_bytes=64)
-            for half in range(2):
-                n_range = slice(half * HALF_N, (half + 1) * HALF_N)
-                dst = win_grouped[:, n_range].rearrange("q n i t -> q i t n")
-                src = win_raws[c][:, :, :, n_range].rearrange("q t i n -> q i t n")
-                if c % 2 == 0:
-                    nc.vector.tensor_copy(out=dst, in_=src)
-                else:
-                    nc.scalar.copy(out=dst, in_=src)
-            win_groupeds[c] = win_grouped
+        def regroup_win(c, half, copy):
+            pair, second = divmod(c, 2)
+            if pair not in win_groupeds:
+                win_groupeds[pair] = wstage.tile(
+                    [P, HN, 2 * I_CHUNK, PACK], BF16, tag="grouped", bufs=2, name="win_grouped", align_bytes=64
+                )
+            n_range = slice(half * HALF_N, (half + 1) * HALF_N)
+            i_range = slice(second * I_CHUNK, (second + 1) * I_CHUNK)
+            copy(
+                out=win_groupeds[pair][:, n_range, i_range].rearrange("q n i t -> q i t n"),
+                in_=win_raws[c][:, :, :, n_range].rearrange("q t i n -> q i t n"),
+            )
 
-        def quantise_win(c):
-            i_cols = slice(c * I_CHUNK, (c + 1) * I_CHUNK)
-            for n in range(HN):
+        def quantise_win(pair, half):
+            i_cols = slice(pair * 2 * I_CHUNK, (pair + 1) * 2 * I_CHUNK)
+            for n in range(half * HALF_N, (half + 1) * HALF_N):
                 nc.vector.quantize_mx(
                     out=win_codes[:, n, i_cols].bitcast(E4M3_X4),
                     scales=win_scales[:, n, i_cols],
-                    in_=win_groupeds[c][:, n].rearrange("q i t -> q (i t)"),
+                    in_=win_groupeds[pair][:, n].rearrange("q i t -> q (i t)"),
                 )
 
         wim_groupeds = {}
 
         def regroup_wim(a):
             wim_words = wim_raws[a][:].rearrange("p c m -> p (c m)").bitcast(F32).rearrange("p (c w) -> p c w", w=HM // 2)
-            wim_grouped = wstage.tile([P, 2 * IN_C * PACK], BF16, tag="grouped", bufs=3, name="wim_grouped", align_bytes=64)
-            grouped_words = wim_grouped[:].bitcast(F32).rearrange("q (i u) -> q i u", u=2)
+            wim_grouped = wstage.tile([P, 2 * IN_C * PACK], BF16, tag="grouped", bufs=2, name="wim_grouped", align_bytes=64)
+            grouped_words = wim_grouped[:].bitcast(F32).rearrange("q (n p cc u) -> q n p cc u", n=2, cc=4, u=2)
             for i_half in range(4):
+                nn, c_half = divmod(i_half, 2)
                 bank = tpsum.tile([P, 2, 2 * P], F32, tag="bank", name="wim_bank")
                 for u in range(2):
                     for cc in range(2):
@@ -135,8 +146,8 @@ def tile_tensormoe_pa_v_kernel(tc, x, W_im, W_in, leak_m, leak_n, z_m, z_n, grad
                             identity=ident[:],
                         )
                 nc.scalar.copy(
-                    out=grouped_words[:, i_half * 2 * P : (i_half + 1) * 2 * P, :],
-                    in_=bank[:].rearrange("q u i -> q i u"),
+                    out=grouped_words[:, nn, :, 2 * c_half : 2 * c_half + 2],
+                    in_=bank[:].rearrange("q u (cc p) -> q p cc u", cc=2),
                 )
             wim_groupeds[a] = wim_grouped
 
@@ -149,6 +160,14 @@ def tile_tensormoe_pa_v_kernel(tc, x, W_im, W_in, leak_m, leak_n, z_m, z_n, grad
 
         lm_minus_1 = const.tile([P, PACK], F32)
         ln_minus_1 = const.tile([P, HN], F32)
+
+        def spread_slopes():
+            lm_bank = tpsum.tile([P, P], F32, tag="bank", name="lm_bank")
+            nc.tensor.transpose(out=lm_bank[:], in_=lm_rows[:].bitcast(F32), identity=ident[:])
+            nc.vector.tensor_scalar_add(out=lm_minus_1[:], in0=lm_bank[:, 0:2].bitcast(BF16), scalar1=-1.0)
+            ln_bank = tpsum.tile([P, HN], F32, tag="bank", name="ln_bank")
+            nc.tensor.matmul(out=ln_bank[:], lhsT=ones[:], rhs=ln_rows[:], start=True, stop=True)
+            nc.vector.tensor_scalar_add(out=ln_minus_1[:], in0=ln_bank[:], scalar1=-1.0)
 
         neg_ns, neg_ms, fns, fms, g_banks, products, codes = {}, {}, {}, {}, {}, {}, {}
         acc_of = {}
@@ -244,6 +263,31 @@ def tile_tensormoe_pa_v_kernel(tc, x, W_im, W_in, leak_m, leak_n, z_m, z_n, grad
                 nc.vector.tensor_tensor(out=dn_view, in0=fn_view, in1=g_view, op=ALU.mult)
                 nc.vector.tensor_tensor(out=dm_view, in0=fm_view, in1=g_view, op=ALU.mult)
 
+        def multiply_and_quantise_last(s):
+            products[s] = (
+                work.tile([P, STAGE * PACK], BF16, name="dnT", bufs=1, align_bytes=64),
+                work.tile([P, STAGE * PACK], BF16, name="dmT", bufs=1, align_bytes=64),
+            )
+            dnT, dmT = products[s]
+            (g0, dn0, fn0, dm0, fm0), (g1, dn1, fn1, dm1, fm1) = pair_views(s, 0), pair_views(s, 1)
+            dn_codes = work.tile([P, STAGE], U32, name="dn_codes", align_bytes=64)
+            dn_scales = work.tile([P, STAGE], U8, name="dn_scales", align_bytes=64)
+            dm_codes = work.tile([P, STAGE], U32, name="dm_codes", align_bytes=64)
+            dm_scales = work.tile([P, STAGE], U8, name="dm_scales", align_bytes=64)
+            nc.vector.tensor_tensor(out=dn0, in0=fn0, in1=g0, op=ALU.mult)
+            nc.vector.tensor_tensor(out=dn1, in0=fn1, in1=g1, op=ALU.mult)
+            nc.vector.quantize_mx(out=dn_codes[:].bitcast(E5M2_X4), scales=dn_scales[:], in_=dnT[:])
+            nc.vector.tensor_tensor(out=dm0, in0=fm0, in1=g0, op=ALU.mult)
+            nc.vector.tensor_tensor(out=dm1, in0=fm1, in1=g1, op=ALU.mult)
+            for pair in range(2):
+                cols = slice(pair * 2 * P, (pair + 1) * 2 * P)
+                nc.vector.quantize_mx(
+                    out=dm_codes[:, cols].bitcast(E5M2_X4),
+                    scales=dm_scales[:, cols],
+                    in_=dmT[:, pair * 2 * P * PACK : (pair + 1) * 2 * P * PACK],
+                )
+            codes[s] = ((dn_codes, dn_scales, win_codes, win_scales), (dm_codes, dm_scales, wim_codes, wim_scales))
+
         def quantise(s):
             dnT, dmT = products[s]
             dn_codes = work.tile([P, STAGE], U32, name="dn_codes", align_bytes=64)
@@ -273,62 +317,69 @@ def tile_tensormoe_pa_v_kernel(tc, x, W_im, W_in, leak_m, leak_n, z_m, z_n, grad
                         start=(h == 0 and product == 0 and nq == 0),
                         stop=(h == 1 and product == 1 and nq == HALF_N - 1),
                     )
-            if h == 1:
-                out_rows = work.tile([P, IN_C], F32, name="out_rows")
-                nc.scalar.copy(out=out_rows[:], in_=acc[:])
-                nc.scalar.dma_start(out=out[j * P : (j + 1) * P, :], in_=out_rows[:])
 
-        for c in range(I_CHUNKS):
+        def store_rows(j):
+            out_rows = work.tile([P, IN_C], F32, name="out_rows")
+            nc.scalar.copy(out=out_rows[:], in_=acc_of[j][:])
+            nc.scalar.dma_start(out=out[j * P : (j + 1) * P, :], in_=out_rows[:])
+
+        by_vector, by_scalar = nc.vector.tensor_copy, nc.scalar.copy
+        for c in range(3):
             load_win(c)
-        regroup_win(0)
-        regroup_win(1)
-        load_wim(0)
-        load_zn_and_g(0)
-        load_wim(1)
         load_zm(0)
-        quantise_win(0)
-        regroup_win(2)
-        load_wim(2)
+        load_win(3)
+        load_zn(0)
+        load_g(0)
+        regroup_win(0, 0, by_vector)
+        regroup_win(0, 1, by_scalar)
+        load_wim(0)
         load_zm(1)
-        quantise_win(2)
-        quantise_win(1)
-        regroup_win(3)
+        regroup_win(1, 0, by_vector)
+        regroup_win(1, 1, by_scalar)
+        load_wim(1)
+        quantise_win(0, 0)
+        regroup_win(2, 0, by_vector)
+        spread_slopes()
+        signs_m(0)
+        quantise_win(0, 1)
+        regroup_win(2, 1, by_scalar)
+        load_wim(2)
+        factors_m(0)
+        regroup_win(3, 0, by_vector)
+        regroup_win(3, 1, by_vector)
         load_wim(3)
-        load_zn_and_g(1)
+        load_zn(1)
         load_zm(2)
-        regroup_wim(0)
-        quantise_win(3)
-        nc.vector.tensor_scalar_add(out=lm_minus_1[:], in0=lm_bf[:], scalar1=-1.0)
-        nc.vector.tensor_scalar_add(out=ln_minus_1[:], in0=ln_bf[:], scalar1=-1.0)
+        load_g(1)
+        quantise_win(1, 0)
         signs_n(0)
         factors_n(0)
-        transpose_g(0)
-        quantise_wim(0)
         signs_n(1)
+        transpose_g(0)
         factors_n(1)
-        signs_m(0)
-        regroup_wim(1)
-        factors_m(0)
         load_behind(0)
-        quantise_wim(1)
-        regroup_wim(2)
-        signs_m(1)
+        quantise_win(1, 1)
+        regroup_wim(0)
         multiply(0)
-        transpose_g(1)
+        signs_m(1)
         factors_m(1)
-        load_behind(1)
         quantise(0)
-        quantise_wim(2)
-        regroup_wim(3)
-        passes(0)
+        transpose_g(1)
+        load_behind(1)
+        regroup_wim(1)
+        quantise_wim(0)
         multiply(1)
+        regroup_wim(2)
         quantise(1)
+        quantise_wim(1)
+        regroup_wim(3)
         signs_n(2)
         factors_n(2)
-        quantise_wim(3)
+        quantise_wim(2)
         signs_m(2)
         factors_m(2)
-        passes(1)
+        quantise_wim(3)
+        passes(0)
         transpose_g(2)
         load_behind(2)
 
@@ -338,11 +389,16 @@ def tile_tensormoe_pa_v_kernel(tc, x, W_im, W_in, leak_m, leak_n, z_m, z_n, grad
                 signs_m(s + 1)
                 factors_n(s + 1)
                 factors_m(s + 1)
-            multiply(s)
-            quantise(s)
-            if s - 1 >= 2:
-                passes(s - 1)
+            if s % 2 == 1:
+                store_rows(s // 2 - 1)
+            if s + 1 < STAGES:
+                multiply(s)
+                quantise(s)
+            else:
+                multiply_and_quantise_last(s)
+            passes(s - 1)
             if s + 1 < STAGES:
                 transpose_g(s + 1)
                 load_behind(s + 1)
         passes(STAGES - 1)
+        store_rows(B_TILES - 1)

@@ -346,7 +346,7 @@ def tile_tensormoe_pa_v_kernel(tc, x, W_im, W_in, leak_m, leak_n, z_m, z_n, grad
         load_wim(2)
         factors_m(0)
         regroup_win(3, 0, by_vector)
-        regroup_win(3, 1, by_vector)
+        regroup_win(3, 1, by_scalar)
         load_wim(3)
         load_zn(1)
         load_zm(2)

@@ -214,21 +214,25 @@ def tile_tensormoe_pa_v_kernel(tc, x, W_im, W_in, leak_m, leak_n, z_m, z_n, grad
         def factors_m(s):
             words_of = neg_ms[s][:].bitcast(F32)
             fms[s] = work.tile([P, 2, STAGE, 2], BF16, name="fmT")
+            banks = []
             for u in range(2):
                 m_bank = tpsum.tile([P, HALF_N, P], F32, tag="bank", name="m_bank")
                 for nq in range(HALF_N):
                     words = slice(nq * 2 * P + u * P, nq * 2 * P + (u + 1) * P)
                     nc.tensor.transpose(out=m_bank[:, nq, :], in_=words_of[:, words], identity=ident[:])
-                m_bank_bf = m_bank[:].rearrange("q nq b -> q (nq b)").bitcast(BF16).rearrange("q (x e) -> q x e", e=2)
-                for e in range(2):
-                    t = 2 * u + e
-                    nc.scalar.activation(
-                        out=fms[s][:, u, :, e],
-                        in_=m_bank_bf[:, :, e],
-                        func=ACT.Copy,
-                        scale=lm_minus_1[:, t : t + 1],
-                        bias=1.0,
-                    )
+                banks.append(m_bank[:].rearrange("q nq b -> q (nq b)").bitcast(BF16).rearrange("q (x e) -> q x e", e=2))
+            width = STAGE if s < STAGES - 1 else STAGE // 2
+            for x in range(0, STAGE, width):
+                for u in range(2):
+                    for e in range(2):
+                        t = 2 * u + e
+                        nc.scalar.activation(
+                            out=fms[s][:, u, x : x + width, e],
+                            in_=banks[u][:, x : x + width, e],
+                            func=ACT.Copy,
+                            scale=lm_minus_1[:, t : t + 1],
+                            bias=1.0,
+                        )
 
         def transpose_g(s):
             j, h = divmod(s, 2)
@@ -274,18 +278,22 @@ def tile_tensormoe_pa_v_kernel(tc, x, W_im, W_in, leak_m, leak_n, z_m, z_n, grad
             dn_scales = work.tile([P, STAGE], U8, name="dn_scales", align_bytes=64)
             dm_codes = work.tile([P, STAGE], U32, name="dm_codes", align_bytes=64)
             dm_scales = work.tile([P, STAGE], U8, name="dm_scales", align_bytes=64)
-            nc.vector.tensor_tensor(out=dn0, in0=fn0, in1=g0, op=ALU.mult)
-            nc.vector.tensor_tensor(out=dn1, in0=fn1, in1=g1, op=ALU.mult)
-            nc.vector.quantize_mx(out=dn_codes[:].bitcast(E5M2_X4), scales=dn_scales[:], in_=dnT[:])
-            nc.vector.tensor_tensor(out=dm0, in0=fm0, in1=g0, op=ALU.mult)
-            nc.vector.tensor_tensor(out=dm1, in0=fm1, in1=g1, op=ALU.mult)
-            for pair in range(2):
+
+            def quantise_dm_pair(pair):
                 cols = slice(pair * 2 * P, (pair + 1) * 2 * P)
                 nc.vector.quantize_mx(
                     out=dm_codes[:, cols].bitcast(E5M2_X4),
                     scales=dm_scales[:, cols],
                     in_=dmT[:, pair * 2 * P * PACK : (pair + 1) * 2 * P * PACK],
                 )
+
+            nc.vector.tensor_tensor(out=dn0, in0=fn0, in1=g0, op=ALU.mult)
+            nc.vector.tensor_tensor(out=dn1, in0=fn1, in1=g1, op=ALU.mult)
+            nc.vector.tensor_tensor(out=dm0, in0=fm0, in1=g0, op=ALU.mult)
+            nc.vector.quantize_mx(out=dn_codes[:].bitcast(E5M2_X4), scales=dn_scales[:], in_=dnT[:])
+            quantise_dm_pair(0)
+            nc.vector.tensor_tensor(out=dm1, in0=fm1, in1=g1, op=ALU.mult)
+            quantise_dm_pair(1)
             codes[s] = ((dn_codes, dn_scales, win_codes, win_scales), (dm_codes, dm_scales, wim_codes, wim_scales))
 
         def quantise(s):

import concourse.mybir as mybir
from concourse.masks import make_identity

F32 = mybir.dt.float32
BF16 = mybir.dt.bfloat16
U32 = mybir.dt.uint32
U8 = mybir.dt.uint8
E4M3_X4 = mybir.dt.float8_e4m3fn_x4
E5M2_X4 = mybir.dt.float8_e5m2_x4
ALU = mybir.AluOpType
ACT = mybir.ActivationFunctionType

P = 128
B, IN_C, HM, HN = 512, 512, 512, 8
PACK = 4
B_TILES = B // P
HALF_N = HN // 2
STAGES = 2 * B_TILES
STAGE = HALF_N * P
I_CHUNKS = 4
I_CHUNK = IN_C // I_CHUNKS
N_PAIRS = HN // 2

FLOPS = 2 * 2 * B * IN_C * HN * HM
BYTES = 2 * (2 * HN * IN_C * HM) + 2 * (4 * B * HN * HM) + 2 * B * HN * HM + 4 * B * IN_C


def tile_tensormoe_pa_v_kernel(tc, x, W_im, W_in, leak_m, leak_n, z_m, z_n, grad_out, out):
    nc = tc.nc
    with (
        tc.tile_pool(name="const", bufs=1) as const,
        tc.tile_pool(name="weights", bufs=1) as weights,
        tc.tile_pool(name="wstage", bufs=2) as wstage,
        tc.tile_pool(name="loads", bufs=2) as loads,
        tc.tile_pool(name="work", bufs=2) as work,
        tc.psum_pool(name="tpsum", bufs=4) as tpsum,
        tc.psum_pool(name="gpsum", bufs=2) as gpsum,
        tc.psum_pool(name="accs", bufs=2) as accs,
        tc.manual_schedule(),
    ):

        ident = const.tile([P, P], F32)
        make_identity(nc, ident[:])
        zero = const.tile([P, 1], F32)
        warm = const.tile([P, 1], F32)
        nc.vector.memset(zero[:], 0.0)
        nc.scalar.copy(out=warm[:], in_=zero[:])
        lm_rows = const.tile([P, 2 * P], BF16)
        ln_rows = const.tile([P, HN], BF16)
        ones = const.tile([P, P], BF16)
        nc.vector.memset(lm_rows[:], 0.0)
        nc.vector.memset(ln_rows[:], 0.0)
        nc.gpsimd.memset(ones[:], 1.0)
        nc.scalar.dma_start(out=lm_rows[0:2, :], in_=leak_m.rearrange("(u w) -> u w", u=2))
        nc.scalar.dma_start(out=ln_rows[0:1, :], in_=leak_n.unsqueeze(0))

        wim_codes = weights.tile([P, HN, IN_C], U32, align_bytes=64)
        wim_scales = weights.tile([P, HN, IN_C], U8, align_bytes=64)
        win_codes = weights.tile([P, HN, IN_C], U32, align_bytes=64)
        win_scales = weights.tile([P, HN, IN_C], U8, align_bytes=64)

        zns, gs = {}, {}
        zms = {}
        win_raws, wim_raws = {}, {}
        win_rows = W_in.rearrange("(u q e) i n -> u q e (i n)", u=2, e=2)

        def load_win(c):
            win_raw = wstage.tile([P, PACK, I_CHUNK, HN], BF16, tag="raw", bufs=4, name="win_raw")
            for u in range(2):
                nc.sync.dma_start(
                    out=win_raw[:, 2 * u : 2 * u + 2].rearrange("q e i n -> q e (i n)"),
                    in_=win_rows[u, :, :, c * I_CHUNK * HN : (c + 1) * I_CHUNK * HN],
                )
            win_raws[c] = win_raw

        def load_wim(a):
            wim_raw = wstage.tile([P, 2 * IN_C // P, HM], BF16, tag="raw", bufs=4, name="wim_raw")
            nc.sync.dma_start(
                out=wim_raw[:].rearrange("p (n c) m -> p n c m", n=2),
                in_=W_im[2 * a : 2 * a + 2].rearrange("n (p c) m -> p n c m", p=P),
            )
            wim_raws[a] = wim_raw

        def load_zn(j):
            rows = slice(j * P, (j + 1) * P)
            zns[j] = loads.tile([P, HM * HN], F32, name="zn")
            nc.sync.dma_start(out=zns[j][:], in_=z_n[rows].rearrange("b m n -> b (m n)"))

        def load_g(j):
            rows = slice(j * P, (j + 1) * P)
            gs[j] = loads.tile([P, HN * HM], BF16, name="g")
            nc.sync.dma_start(out=gs[j][:], in_=grad_out[rows].rearrange("b n m -> b (n m)"))

        def load_zm(s):
            j, h = divmod(s, 2)
            zms[s] = loads.tile([P, HALF_N * HM], F32, name="zm", bufs=3)
            n_range = slice(h * HALF_N, (h + 1) * HALF_N)
            nc.sync.dma_start(out=zms[s][:], in_=z_m[j * P : (j + 1) * P, n_range, :].rearrange("b n m -> b (n m)"))

        def load_behind(s):
            if s % 2 == 1 and (s + 3) // 2 < B_TILES:
                load_zn((s + 3) // 2)
            if s + 3 < STAGES:
                load_zm(s + 3)
            if s % 2 == 1 and (s + 3) // 2 < B_TILES:
                load_g((s + 3) // 2)

        win_groupeds = {}

        def regroup_win(c, half, copy):
            pair, second = divmod(c, 2)
            if pair not in win_groupeds:
                win_groupeds[pair] = wstage.tile(
                    [P, HN, 2 * I_CHUNK, PACK], BF16, tag="grouped", bufs=2, name="win_grouped", align_bytes=64
                )
            n_range = slice(half * HALF_N, (half + 1) * HALF_N)
            i_range = slice(second * I_CHUNK, (second + 1) * I_CHUNK)
            copy(
                out=win_groupeds[pair][:, n_range, i_range].rearrange("q n i t -> q i t n"),
                in_=win_raws[c][:, :, :, n_range].rearrange("q t i n -> q i t n"),
            )

        def quantise_win(pair, half):
            i_cols = slice(pair * 2 * I_CHUNK, (pair + 1) * 2 * I_CHUNK)
            for n in range(half * HALF_N, (half + 1) * HALF_N):
                nc.vector.quantize_mx(
                    out=win_codes[:, n, i_cols].bitcast(E4M3_X4),
                    scales=win_scales[:, n, i_cols],
                    in_=win_groupeds[pair][:, n].rearrange("q i t -> q (i t)"),
                )

        wim_groupeds = {}

        def regroup_wim(a):
            wim_words = wim_raws[a][:].rearrange("p c m -> p (c m)").bitcast(F32).rearrange("p (c w) -> p c w", w=HM // 2)
            wim_grouped = wstage.tile([P, 2 * IN_C * PACK], BF16, tag="grouped", bufs=2, name="wim_grouped", align_bytes=64)
            grouped_words = wim_grouped[:].bitcast(F32).rearrange("q (n p cc u) -> q n p cc u", n=2, cc=4, u=2)
            for i_half in range(4):
                nn, c_half = divmod(i_half, 2)
                bank = tpsum.tile([P, 2, 2 * P], F32, tag="bank", name="wim_bank")
                for u in range(2):
                    for cc in range(2):
                        nc.tensor.transpose(
                            out=bank[:, u, cc * P : (cc + 1) * P],
                            in_=wim_words[:, 2 * i_half + cc, u * P : (u + 1) * P],
                            identity=ident[:],
                        )
                nc.scalar.copy(
                    out=grouped_words[:, nn, :, 2 * c_half : 2 * c_half + 2],
                    in_=bank[:].rearrange("q u (cc p) -> q p cc u", cc=2),
                )
            wim_groupeds[a] = wim_grouped

        def quantise_wim(a):
            nc.vector.quantize_mx(
                out=wim_codes[:, 2 * a : 2 * a + 2, :].rearrange("q n i -> q (n i)").bitcast(E4M3_X4),
                scales=wim_scales[:, 2 * a : 2 * a + 2, :].rearrange("q n i -> q (n i)"),
                in_=wim_groupeds[a][:],
            )

        lm_minus_1 = const.tile([P, PACK], F32)
        ln_minus_1 = const.tile([P, HN], F32)

        def spread_slopes():
            lm_bank = tpsum.tile([P, P], F32, tag="bank", name="lm_bank")
            nc.tensor.transpose(out=lm_bank[:], in_=lm_rows[:].bitcast(F32), identity=ident[:])
            nc.vector.tensor_scalar_add(out=lm_minus_1[:], in0=lm_bank[:, 0:2].bitcast(BF16), scalar1=-1.0)
            ln_bank = tpsum.tile([P, HN], F32, tag="bank", name="ln_bank")
            nc.tensor.matmul(out=ln_bank[:], lhsT=ones[:], rhs=ln_rows[:], start=True, stop=True)
            nc.vector.tensor_scalar_add(out=ln_minus_1[:], in0=ln_bank[:], scalar1=-1.0)

        neg_ns, neg_ms, fns, fms, g_banks, products, codes = {}, {}, {}, {}, {}, {}, {}
        acc_of = {}

        def signs_n(s):
            j, h = divmod(s, 2)
            neg_ns[s] = work.tile([P, HALF_N, HM], BF16, name="neg_n")
            nc.vector.tensor_single_scalar(
                out=neg_ns[s][:].rearrange("b nq m -> b m nq"),
                in_=zns[j][:].rearrange("b (m hh nq) -> b hh m nq", hh=2, nq=HALF_N)[:, h],
                scalar=0.0,
                op=ALU.is_lt,
            )

        def signs_m(s):
            neg_ms[s] = work.tile([P, HALF_N * HM], BF16, name="neg_m")
            nc.vector.tensor_single_scalar(out=neg_ms[s][:], in_=zms[s][:], scalar=0.0, op=ALU.is_lt)

        def factors_n(s):
            h = s % 2
            words_of = neg_ns[s][:].rearrange("b nq m -> b (nq m)").bitcast(F32)
            fns[s] = work.tile([P, STAGE * PACK], BF16, name="fnT")
            fnT_view = fns[s][:].rearrange("q (nq b u e) -> q nq b u e", nq=HALF_N, u=2, e=2)
            for pair in range(HALF_N // 2):
                n_bank = tpsum.tile([P, 2, 2, P], F32, tag="bank", name="n_bank")
                for nn in range(2):
                    nq = 2 * pair + nn
                    for u in range(2):
                        words = slice(nq * 2 * P + u * P, nq * 2 * P + (u + 1) * P)
                        nc.tensor.transpose(out=n_bank[:, nn, u, :], in_=words_of[:, words], identity=ident[:])
                n_bank_bf = n_bank[:].rearrange("q nn u b -> q (nn u b)").bitcast(BF16).rearrange(
                    "q (nn u b e) -> q nn b u e", nn=2, u=2, e=2
                )
                for nn in range(2):
                    n = h * HALF_N + 2 * pair + nn
                    nc.scalar.activation(
                        out=fnT_view[:, 2 * pair + nn],
                        in_=n_bank_bf[:, nn],
                        func=ACT.Copy,
                        scale=ln_minus_1[:, n : n + 1],
                        bias=1.0,
                    )

        def factors_m(s):
            words_of = neg_ms[s][:].bitcast(F32)
            fms[s] = work.tile([P, 2, STAGE, 2], BF16, name="fmT")
            banks = []
            for u in range(2):
                m_bank = tpsum.tile([P, HALF_N, P], F32, tag="bank", name="m_bank")
                for nq in range(HALF_N):
                    words = slice(nq * 2 * P + u * P, nq * 2 * P + (u + 1) * P)
                    nc.tensor.transpose(out=m_bank[:, nq, :], in_=words_of[:, words], identity=ident[:])
                banks.append(m_bank[:].rearrange("q nq b -> q (nq b)").bitcast(BF16).rearrange("q (x e) -> q x e", e=2))
            width = STAGE if s < STAGES - 1 else STAGE // 2
            for x in range(0, STAGE, width):
                for u in range(2):
                    for e in range(2):
                        t = 2 * u + e
                        nc.scalar.activation(
                            out=fms[s][:, u, x : x + width, e],
                            in_=banks[u][:, x : x + width, e],
                            func=ACT.Copy,
                            scale=lm_minus_1[:, t : t + 1],
                            bias=1.0,
                        )

        def transpose_g(s):
            j, h = divmod(s, 2)
            g_words = gs[j][:].bitcast(F32)
            g_banks[s] = []
            for pair in range(HALF_N // 2):
                g_bank = gpsum.tile([P, 2, 2 * P], F32, name="g_bank")
                for nn in range(2):
                    n = h * HALF_N + 2 * pair + nn
                    for u in range(2):
                        words = slice(n * 2 * P + u * P, n * 2 * P + (u + 1) * P)
                        nc.tensor.transpose(out=g_bank[:, u, nn * P : (nn + 1) * P], in_=g_words[:, words], identity=ident[:])
                g_banks[s].append(g_bank)

        def pair_views(s, pair):
            dnT, dmT = products[s]
            two = slice(2 * P * pair, 2 * P * (pair + 1))
            g_view = g_banks[s][pair][:].rearrange("q u x -> q (u x)").bitcast(BF16).rearrange("q (u x e) -> q x u e", u=2, e=2)
            dn_view = dnT[:].rearrange("q (x u e) -> q x u e", u=2, e=2)[:, two]
            dm_view = dmT[:].rearrange("q (x u e) -> q x u e", u=2, e=2)[:, two]
            fn_view = fns[s][:].rearrange("q (x u e) -> q x u e", u=2, e=2)[:, two]
            fm_view = fms[s][:].rearrange("q u x e -> q x u e")[:, two]
            return g_view, dn_view, fn_view, dm_view, fm_view

        def multiply(s):
            products[s] = (
                work.tile([P, STAGE * PACK], BF16, name="dnT", bufs=1, align_bytes=64),
                work.tile([P, STAGE * PACK], BF16, name="dmT", bufs=1, align_bytes=64),
            )
            for pair in range(HALF_N // 2):
                g_view, dn_view, fn_view, dm_view, fm_view = pair_views(s, pair)
                nc.vector.tensor_tensor(out=dn_view, in0=fn_view, in1=g_view, op=ALU.mult)
                nc.vector.tensor_tensor(out=dm_view, in0=fm_view, in1=g_view, op=ALU.mult)

        def multiply_and_quantise_last(s):
            products[s] = (
                work.tile([P, STAGE * PACK], BF16, name="dnT", bufs=1, align_bytes=64),
                work.tile([P, STAGE * PACK], BF16, name="dmT", bufs=1, align_bytes=64),
            )
            dnT, dmT = products[s]
            (g0, dn0, fn0, dm0, fm0), (g1, dn1, fn1, dm1, fm1) = pair_views(s, 0), pair_views(s, 1)
            dn_codes = work.tile([P, STAGE], U32, name="dn_codes", align_bytes=64)
            dn_scales = work.tile([P, STAGE], U8, name="dn_scales", align_bytes=64)
            dm_codes = work.tile([P, STAGE], U32, name="dm_codes", align_bytes=64)
            dm_scales = work.tile([P, STAGE], U8, name="dm_scales", align_bytes=64)

            def quantise_dm_pair(pair):
                cols = slice(pair * 2 * P, (pair + 1) * 2 * P)
                nc.vector.quantize_mx(
                    out=dm_codes[:, cols].bitcast(E5M2_X4),
                    scales=dm_scales[:, cols],
                    in_=dmT[:, pair * 2 * P * PACK : (pair + 1) * 2 * P * PACK],
                )

            nc.vector.tensor_tensor(out=dn0, in0=fn0, in1=g0, op=ALU.mult)
            nc.vector.tensor_tensor(out=dn1, in0=fn1, in1=g1, op=ALU.mult)
            nc.vector.tensor_tensor(out=dm0, in0=fm0, in1=g0, op=ALU.mult)
            nc.vector.quantize_mx(out=dn_codes[:].bitcast(E5M2_X4), scales=dn_scales[:], in_=dnT[:])
            quantise_dm_pair(0)
            nc.vector.tensor_tensor(out=dm1, in0=fm1, in1=g1, op=ALU.mult)
            quantise_dm_pair(1)
            codes[s] = ((dn_codes, dn_scales, win_codes, win_scales), (dm_codes, dm_scales, wim_codes, wim_scales))

        def quantise(s):
            dnT, dmT = products[s]
            dn_codes = work.tile([P, STAGE], U32, name="dn_codes", align_bytes=64)
            dn_scales = work.tile([P, STAGE], U8, name="dn_scales", align_bytes=64)
            dm_codes = work.tile([P, STAGE], U32, name="dm_codes", align_bytes=64)
            dm_scales = work.tile([P, STAGE], U8, name="dm_scales", align_bytes=64)
            nc.vector.quantize_mx(out=dn_codes[:].bitcast(E5M2_X4), scales=dn_scales[:], in_=dnT[:])
            nc.vector.quantize_mx(out=dm_codes[:].bitcast(E5M2_X4), scales=dm_scales[:], in_=dmT[:])
            codes[s] = ((dn_codes, dn_scales, win_codes, win_scales), (dm_codes, dm_scales, wim_codes, wim_scales))

        def passes(s):
            j, h = divmod(s, 2)
            if h == 0:
                acc_of[j] = accs.tile([P, IN_C], F32, name="acc")
            acc = acc_of[j]
            for product in range(2):
                d_codes, d_scales, w_codes, w_scales = codes[s][product]
                for nq in range(HALF_N):
                    n = h * HALF_N + nq
                    b_cols = slice(nq * P, (nq + 1) * P)
                    nc.tensor.matmul_mx(
                        out=acc[:],
                        lhsT=d_codes[:, b_cols].bitcast(E5M2_X4),
                        lhsT_scale=d_scales[:, b_cols],
                        rhs=w_codes[:, n, :].bitcast(E4M3_X4),
                        rhs_scale=w_scales[:, n, :],
                        start=(h == 0 and product == 0 and nq == 0),
                        stop=(h == 1 and product == 1 and nq == HALF_N - 1),
                    )

        def store_rows(j):
            out_rows = work.tile([P, IN_C], F32, name="out_rows")
            nc.scalar.copy(out=out_rows[:], in_=acc_of[j][:])
            nc.scalar.dma_start(out=out[j * P : (j + 1) * P, :], in_=out_rows[:])

        by_vector, by_scalar = nc.vector.tensor_copy, nc.scalar.copy
        for c in range(3):
            load_win(c)
        load_zm(0)
        load_win(3)
        load_zn(0)
        load_g(0)
        regroup_win(0, 0, by_vector)
        regroup_win(0, 1, by_scalar)
        load_wim(0)
        load_zm(1)
        regroup_win(1, 0, by_vector)
        regroup_win(1, 1, by_scalar)
        load_wim(1)
        quantise_win(0, 0)
        regroup_win(2, 0, by_vector)
        spread_slopes()
        signs_m(0)
        quantise_win(0, 1)
        regroup_win(2, 1, by_scalar)
        load_wim(2)
        factors_m(0)
        regroup_win(3, 0, by_vector)
        regroup_win(3, 1, by_scalar)
        load_wim(3)
        load_zn(1)
        load_zm(2)
        load_g(1)
        quantise_win(1, 0)
        signs_n(0)
        factors_n(0)
        signs_n(1)
        transpose_g(0)
        factors_n(1)
        load_behind(0)
        quantise_win(1, 1)
        regroup_wim(0)
        multiply(0)
        signs_m(1)
        factors_m(1)
        quantise(0)
        transpose_g(1)
        load_behind(1)
        regroup_wim(1)
        quantise_wim(0)
        multiply(1)
        regroup_wim(2)
        quantise(1)
        quantise_wim(1)
        regroup_wim(3)
        signs_n(2)
        factors_n(2)
        quantise_wim(2)
        signs_m(2)
        factors_m(2)
        quantise_wim(3)
        passes(0)
        transpose_g(2)
        load_behind(2)

        for s in range(2, STAGES):
            if s + 1 < STAGES:
                signs_n(s + 1)
                signs_m(s + 1)
                factors_n(s + 1)
                factors_m(s + 1)
            if s % 2 == 1:
                store_rows(s // 2 - 1)
            if s + 1 < STAGES:
                multiply(s)
                quantise(s)
            else:
                multiply_and_quantise_last(s)
            passes(s - 1)
            if s + 1 < STAGES:
                transpose_g(s + 1)
                load_behind(s + 1)
        passes(STAGES - 1)
        store_rows(B_TILES - 1)
